import numpy as np
import ml_dtypes


def mxq(x, axis, fmt="e4m3"):
    dtype, down = {"e4m3": (ml_dtypes.float8_e4m3fn, 7), "e5m2": (ml_dtypes.float8_e5m2, 14)}[fmt]
    v = np.moveaxis(np.asarray(x, np.float32).astype(ml_dtypes.bfloat16).astype(np.float64), axis, -1)
    blocks = v.reshape(v.shape[:-1] + (-1, 32))
    amax = np.abs(blocks).max(-1, keepdims=True)
    byte = np.maximum(np.where(amax > 0, np.frexp(amax)[1] - 1 + 127, 0) - down, 1)
    scale = np.exp2(byte - 127.0)
    codes = (blocks / scale).astype(np.float32).astype(dtype).astype(np.float64)
    return np.moveaxis((codes * scale).reshape(v.shape), -1, axis)


WIDE = False


def mx_kscale(k):
    if not WIDE:
        return np.ones(k)
    levels = np.array([10, -10, 5, -5, 0])
    a = np.random.permutation(np.resize(levels, k // 512 * 4)).reshape(k // 512, 4)
    idx = np.arange(k)
    return np.exp2(a[idx // 512, idx % 128 // 32])


BF16 = ml_dtypes.bfloat16


def bf(x):
    return np.asarray(x, np.float32).astype(BF16)


def f64(x):
    return np.asarray(x).astype(np.float64)


A, L, B, V, D = 128, 32, 128, 16, 512
TAU = 100.0
EPS = 1e-6


def _norm(a):
    n = np.sqrt(np.sum(a * a, axis=-1, keepdims=True))
    return a / np.maximum(n, EPS)


def softmax(z, axis):
    e = np.exp(z - z.max(axis=axis, keepdims=True))
    return e / e.sum(axis=axis, keepdims=True)


def setup_inputs():
    s = mx_kscale(D)
    lens = np.random.randint(L // 2, L + 1, size=A)
    mask = (np.arange(L)[None, :] < lens[:, None]).astype(np.float64)
    c = 2.0 ** np.round(0.5 * np.log2(np.mean(s * s) * np.mean(1.0 / (s * s))))
    return {"text_feat": bf(np.random.standard_normal((A, L, D)) * s), "video_feat": bf(np.random.standard_normal((B, V, D)) / s), "text_mask": bf(mask * c)}


def reference(text_feat, video_feat, text_mask):
    tf = _norm(f64(text_feat))
    vf = _norm(f64(video_feat))
    tq = mxq(tf, 2, "e4m3").reshape(A * L, D)
    vq = mxq(vf, 2, "e4m3").reshape(B * V, D)
    r = (tq @ vq.T).reshape(A, L, B, V).transpose(0, 2, 1, 3)
    r = r * f64(text_mask)[:, None, :, None]
    ps1 = softmax(r * TAU, -1)
    t2v = np.sum(r * ps1, axis=-1)
    ps2 = softmax(np.where(r == 0, -np.inf, r) * TAU, -2)
    v2t = np.sum(r * ps2, axis=-2)
    ps3 = softmax(np.where(t2v == 0, -np.inf, t2v) * TAU, -1)
    t2v_ab = np.sum(t2v * ps3, axis=2)
    ps4 = softmax(v2t * TAU, -1)
    v2t_ab = np.sum(v2t * ps4, axis=2)
    return (t2v_ab + v2t_ab) / 2.0

@@ -1,0 +1,481 @@
+from contextlib import ExitStack
+
+import concourse.mybir as mybir
+from concourse.masks import make_identity
+
+F32 = mybir.dt.float32
+BF16 = mybir.dt.bfloat16
+U32 = mybir.dt.uint32
+U8 = mybir.dt.uint8
+FP8X4 = mybir.dt.float8_e4m3fn_x4
+ALU = mybir.AluOpType
+FN = mybir.ActivationFunctionType
+INNERMOST = mybir.AxisListType.X
+
+P = 128
+TOKENS = 32
+FRAMES = 16
+FEATURES = 512
+PACK = 4
+TAU = 100.0
+EPS = 1.0e-6
+BARRED = -1.0e30
+
+GROUPS = 4
+GROUP_VIDEOS = P // GROUPS
+GROUP_COLS = FRAMES * GROUP_VIDEOS
+BLOCKS = GROUP_COLS // P
+QUAD = 4
+QUADS = TOKENS // QUAD
+FRAME_SUM_COLS = GROUPS * QUADS * P
+SUM_COLS = FRAME_SUM_COLS + GROUPS * GROUP_COLS
+
+FIRST_STEPS = GROUPS * TOKENS
+STEPS = FIRST_STEPS + TOKENS
+DRAIN = 2
+
+FLOPS = 2 * (P * TOKENS) * (P * FRAMES) * FEATURES
+
+
+def tile_mug_head_kernel(tc, text_feat, video_feat, text_mask, out):
+    nc = tc.nc
+    with ExitStack() as pools:
+        consts = pools.enter_context(tc.tile_pool(name="consts", bufs=1))
+        keep = pools.enter_context(tc.tile_pool(name="keep", bufs=1))
+        quad_work = pools.enter_context(tc.tile_pool(name="quad_work", bufs=2))
+        token_work = pools.enter_context(tc.tile_pool(name="token_work", bufs=4))
+        psum = pools.enter_context(tc.psum_pool(name="psum", bufs=2))
+
+        ident_f32 = consts.tile([P, P], F32, name="ident_f32")
+        make_identity(nc, ident_f32[:])
+        ident_bf16 = consts.tile([P, P], BF16, name="ident_bf16")
+        make_identity(nc, ident_bf16[:])
+
+        mask_bf16 = consts.tile([P, TOKENS], BF16, name="mask_bf16")
+        nc.sync.dma_start(out=mask_bf16[:], in_=text_mask)
+        mask = consts.tile([P, TOKENS], F32, name="mask")
+        nc.vector.tensor_copy(out=mask[:], in_=mask_bf16[:])
+        sharp_mask = consts.tile([P, TOKENS], F32, name="sharp_mask")
+        nc.vector.tensor_scalar_mul(out=sharp_mask[:], in0=mask[:], scalar1=TAU)
+        barred = consts.tile([P, TOKENS], F32, name="barred")
+        nc.vector.tensor_scalar(
+            out=barred[:], in0=mask[:], scalar1=0.0, scalar2=BARRED, op0=ALU.is_equal, op1=ALU.mult
+        )
+        mask_top = consts.tile([P, 1], F32, name="mask_top")
+        nc.vector.tensor_reduce(out=mask_top[:], in_=mask[:], axis=INNERMOST, op=ALU.max)
+
+        text_codes = keep.tile([P, TOKENS * P], U32, name="text_codes", align_bytes=64)
+        text_scales = keep.tile([P, TOKENS * P], U8, name="text_scales", align_bytes=64)
+        video_codes = keep.tile([P, GROUPS * GROUP_COLS], U32, name="video_codes", align_bytes=64)
+        video_scales = keep.tile([P, GROUPS * GROUP_COLS], U8, name="video_scales", align_bytes=64)
+        frame_top = keep.tile([P, GROUPS, TOKENS, GROUP_VIDEOS], F32, name="frame_top")
+        token_top = keep.tile([P, GROUPS, GROUP_COLS], F32, name="token_top")
+        sums = keep.tile([P, 2, SUM_COLS], F32, name="sums")
+        text_to_video = keep.tile([P, P], F32, name="text_to_video")
+        video_to_text = keep.tile([P, P], F32, name="video_to_text")
+
+        def transpose_add(acc, block, start, stop):
+            nc.tensor.matmul(
+                out=acc, lhsT=block, rhs=ident_f32[:], is_transpose=True, start=start, stop=stop
+            )
+
+        def inverse_norm(square_sum, inverse):
+            nc.vector.tensor_scalar_max(out=square_sum, in0=square_sum, scalar1=EPS * EPS)
+            nc.scalar.sqrt(out=inverse, in_=square_sum)
+            nc.vector.reciprocal(out=inverse, in_=inverse)
+
+        def features_to_partitions(rows):
+            bank = psum.tile([P, PACK, P], BF16, tag="second", name="turned_rows")
+            for j in range(PACK):
+                nc.tensor.transpose(bank[:, j, :], rows[:, j * P : (j + 1) * P], ident_bf16[:])
+            return bank
+
+        def similarities(token, group, tag):
+            sim = psum.tile([P, GROUP_COLS], F32, tag=tag, name="sim")
+            texts = slice(token * P, (token + 1) * P)
+            cols = slice(group * GROUP_COLS, (group + 1) * GROUP_COLS)
+            nc.tensor.matmul_mx(
+                out=sim[:],
+                lhsT=text_codes[:, texts].bitcast(FP8X4),
+                lhsT_scale=text_scales[:, texts],
+                rhs=video_codes[:, cols].bitcast(FP8X4),
+                rhs_scale=video_scales[:, cols],
+                start=True,
+                stop=True,
+            )
+            return sim
+
+        sim_first = {}
+        sim_second = {}
+        frame_tiles = {}
+        token_tiles = {}
+        quad_banks = {}
+        group_banks = {}
+
+        def in_first_sweep(step):
+            return 0 <= step < FIRST_STEPS
+
+        def in_second_sweep(step):
+            return TOKENS <= step < STEPS
+
+        def multiply(step):
+            token = step % TOKENS
+            if in_first_sweep(step):
+                sim_first[step] = similarities(token, step // TOKENS, "first")
+            if in_second_sweep(step):
+                sim_second[step] = similarities(token, step // TOKENS - 1, "second")
+
+        def subtract_tops(step):
+            token = step % TOKENS
+            if in_second_sweep(step):
+                dev_t = token_work.tile([P, GROUP_COLS], F32, tag="dev_t", name="dev_t")
+                wgt_t = token_work.tile([P, GROUP_COLS], F32, tag="wgt_t", name="wgt_t")
+                token_tiles[step] = (dev_t, wgt_t)
+                nc.vector.scalar_tensor_tensor(
+                    out=dev_t[:],
+                    in0=sim_second[step][:],
+                    scalar=mask[:, token : token + 1],
+                    in1=token_top[:, step // TOKENS - 1, :],
+                    op0=ALU.mult,
+                    op1=ALU.subtract,
+                )
+            if in_first_sweep(step):
+                group = step // TOKENS
+                sim = sim_first[step]
+                if step % QUAD == 0:
+                    quad_shape = [P, FRAMES, QUAD, GROUP_VIDEOS]
+                    frame_tiles[step // QUAD] = (
+                        quad_work.tile(quad_shape, F32, tag="dev_f", name="dev_f"),
+                        quad_work.tile(quad_shape, F32, tag="wgt_f", name="wgt_f"),
+                    )
+                dev_f = frame_tiles[step // QUAD][0]
+                top_f = frame_top[:, group, token, :]
+                nc.vector.tensor_reduce(
+                    out=top_f,
+                    in_=sim[:].rearrange("a (v b) -> a b v", v=FRAMES),
+                    axis=INNERMOST,
+                    op=ALU.max,
+                )
+                nc.vector.tensor_tensor(
+                    out=dev_f[:, :, step % QUAD, :],
+                    in0=sim[:].rearrange("a (v b) -> a v b", v=FRAMES),
+                    in1=top_f.unsqueeze(1).to_broadcast([P, FRAMES, GROUP_VIDEOS]),
+                    op=ALU.subtract,
+                )
+                bar = barred[:, token : token + 1]
+                top_t = token_top[:, group, :]
+                if token == 0:
+                    nc.vector.tensor_scalar(
+                        out=top_t, in0=sim[:], scalar1=bar, scalar2=None, op0=ALU.add
+                    )
+                else:
+                    nc.vector.scalar_tensor_tensor(
+                        out=top_t, in0=sim[:], scalar=bar, in1=top_t, op0=ALU.add, op1=ALU.max
+                    )
+                if token == TOKENS - 1:
+                    nc.vector.tensor_scalar_mul(out=top_t, in0=top_t, scalar1=mask_top[:, 0:1])
+
+        def weigh(step):
+            token = step % TOKENS
+            if in_second_sweep(step):
+                dev_t, wgt_t = token_tiles[step]
+                nc.scalar.activation(
+                    out=wgt_t[:],
+                    in_=dev_t[:],
+                    func=FN.Exp,
+                    scale=TAU,
+                    bias=barred[:, token : token + 1],
+                )
+            if in_first_sweep(step):
+                dev_f, wgt_f = frame_tiles[step // QUAD]
+                nc.scalar.activation(
+                    out=wgt_f[:, :, step % QUAD, :],
+                    in_=dev_f[:, :, step % QUAD, :],
+                    func=FN.Exp,
+                    scale=sharp_mask[:, token : token + 1],
+                )
+
+        def form_products(step):
+            if in_second_sweep(step):
+                dev_t, wgt_t = token_tiles[step]
+                nc.gpsimd.tensor_tensor(out=dev_t[:], in0=dev_t[:], in1=wgt_t[:], op=ALU.mult)
+            if in_first_sweep(step):
+                dev_f, wgt_f = frame_tiles[step // QUAD]
+                slot = step % QUAD
+                nc.gpsimd.tensor_tensor(
+                    out=dev_f[:, :, slot, :],
+                    in0=dev_f[:, :, slot, :],
+                    in1=wgt_f[:, :, slot, :],
+                    op=ALU.mult,
+                )
+
+        def add_up_tokens(step):
+            if not in_second_sweep(step):
+                return
+            token = step % TOKENS
+            group = step // TOKENS - 1
+            if token == 0:
+                group_banks[group] = (
+                    psum.tile([P, GROUP_COLS], F32, tag="weight_sums", name="weight_sums", bufs=1),
+                    psum.tile([P, GROUP_COLS], F32, tag="product_sums", name="product_sums", bufs=1),
+                )
+            dev_t, wgt_t = token_tiles[step]
+            for acc, terms in zip(group_banks[group], (wgt_t, dev_t)):
+                for k in range(BLOCKS):
+                    cols = slice(k * P, (k + 1) * P)
+                    transpose_add(
+                        acc[:, cols],
+                        terms[:, cols],
+                        token == 0 and k == 0,
+                        token == TOKENS - 1 and k == BLOCKS - 1,
+                    )
+            if token == TOKENS - 1:
+                first_col = FRAME_SUM_COLS + group * GROUP_COLS
+                for plane, acc in enumerate(group_banks[group]):
+                    nc.scalar.copy(out=sums[:, plane, first_col : first_col + GROUP_COLS], in_=acc[:])
+
+        def add_up_frames(step):
+            if not in_first_sweep(step):
+                return
+            quad = step // QUAD
+            plane = (step % QUAD) // 2
+            first_frame = (step % 2) * (FRAMES // 2)
+            if step % QUAD == 0:
+                quad_banks[quad] = psum.tile([P, 2, P], F32, tag="quad_sums", name="quad_sums")
+            terms = frame_tiles[quad][1 - plane]
+            for v in range(first_frame, first_frame + FRAMES // 2):
+                transpose_add(
+                    quad_banks[quad][:, plane, :],
+                    terms[:, v, :, :].rearrange("a s b -> a (s b)"),
+                    v == 0,
+                    v == FRAMES - 1,
+                )
+
+        def store_frame_sums(step):
+            if in_first_sweep(step) and step % QUAD == QUAD - 1:
+                quad = step // QUAD
+                nc.scalar.copy(out=sums[:, :, quad * P : (quad + 1) * P], in_=quad_banks[quad][:])
+
+        def pipeline_step(step):
+            multiply(step + 1)
+            subtract_tops(step)
+            weigh(step)
+            form_products(step - 1)
+            add_up_tokens(step - 2)
+            add_up_frames(step - QUAD)
+            store_frame_sums(step - QUAD - 1)
+
+        with tc.tile_pool(name="prep", bufs=2) as prep:
+            video_raw = prep.tile([P, FRAMES, FEATURES], BF16, name="video_raw", bufs=1)
+            nc.sync.dma_start(out=video_raw[:], in_=video_feat)
+            text_raw = prep.tile([P, TOKENS, FEATURES], BF16, name="text_raw", bufs=1)
+            for first in range(0, TOKENS, 8):
+                nc.sync.dma_start(
+                    out=text_raw[:, first : first + 8, :], in_=text_feat[:, first : first + 8, :]
+                )
+
+            warm = prep.tile([P, 1], F32, name="warm", bufs=1)
+            nc.vector.memset(warm[:], 1.0)
+            nc.scalar.sqrt(out=warm[:], in_=warm[:])
+
+            def square_sum_on_scalar(rows, total):
+                squares = prep.tile([P, FEATURES], BF16, tag="squares_s", name="squares_s")
+                nc.scalar.activation(out=squares[:], in_=rows, func=FN.Square, accum_out=total)
+
+            def square_sum_on_vector(rows, total):
+                squares = prep.tile([P, FEATURES], F32, tag="squares_v", name="squares_v")
+                nc.vector.scalar_tensor_tensor(
+                    out=squares[:], in0=rows, scalar=1.0, in1=rows,
+                    op0=ALU.mult, op1=ALU.mult, accum_out=total,
+                )
+
+            half = TOKENS // 2
+            video_squares = prep.tile([P, FRAMES], F32, name="video_squares", bufs=1)
+            text_squares_s = prep.tile([P, half], F32, name="text_squares_s", bufs=1)
+            text_squares_v = prep.tile([P, half], F32, name="text_squares_v", bufs=1)
+            video_inverse = prep.tile([P, FRAMES], F32, name="video_inverse", bufs=1)
+            text_inverse = prep.tile([P, TOKENS], F32, name="text_inverse", bufs=1)
+
+            for v in range(FRAMES):
+                square_sum_on_scalar(video_raw[:, v, :], video_squares[:, v : v + 1])
+            inverse_norm(video_squares[:], video_inverse[:])
+
+            video_grouped = prep.tile(
+                [P, GROUPS, FRAMES, GROUP_VIDEOS, PACK], BF16,
+                name="video_grouped", bufs=1, align_bytes=64,
+            )
+            for v in range(FRAMES):
+                rows = prep.tile([P, FEATURES], BF16, tag="rows", name="rows", bufs=3)
+                nc.vector.tensor_scalar_mul(
+                    out=rows[:], in0=video_raw[:, v, :], scalar1=video_inverse[:, v : v + 1]
+                )
+                bank = features_to_partitions(rows)
+                copy = nc.scalar.copy if v % 2 == 0 else nc.vector.tensor_copy
+                copy(
+                    out=video_grouped[:, :, v, :, :],
+                    in_=bank[:].rearrange("p j (g b) -> p g b j", g=GROUPS),
+                )
+            for group in range(GROUPS):
+                cols = slice(group * GROUP_COLS, (group + 1) * GROUP_COLS)
+                nc.vector.quantize_mx(
+                    out=video_codes[:, cols].bitcast(FP8X4),
+                    scales=video_scales[:, cols],
+                    in_=video_grouped[:, group, :, :, :].rearrange("p v b j -> p (v b j)"),
+                )
+
+            for token in range(half):
+                square_sum_on_scalar(text_raw[:, token, :], text_squares_s[:, token : token + 1])
+                square_sum_on_vector(
+                    text_raw[:, half + token, :], text_squares_v[:, token : token + 1]
+                )
+            inverse_norm(text_squares_s[:], text_inverse[:, 0:half])
+            inverse_norm(text_squares_v[:], text_inverse[:, half:TOKENS])
+
+            def prepare_text_quad(quad):
+                grouped = prep.tile(
+                    [P, QUAD, P, PACK], BF16, tag="text_grouped", name="text_grouped", align_bytes=64
+                )
+                for slot in range(QUAD):
+                    token = quad * QUAD + slot
+                    rows = prep.tile([P, FEATURES], BF16, tag="rows", name="rows", bufs=3)
+                    nc.scalar.activation(
+                        out=rows[:],
+                        in_=text_raw[:, token, :],
+                        func=FN.Copy,
+                        scale=text_inverse[:, token : token + 1],
+                    )
+                    bank = features_to_partitions(rows)
+                    nc.scalar.copy(
+                        out=grouped[:, slot, :, :], in_=bank[:].rearrange("p j a -> p a j")
+                    )
+                cols = slice(quad * QUAD * P, (quad + 1) * QUAD * P)
+                nc.vector.quantize_mx(
+                    out=text_codes[:, cols].bitcast(FP8X4),
+                    scales=text_scales[:, cols],
+                    in_=grouped[:].rearrange("p s a j -> p (s a j)"),
+                )
+
+            prepare_text_quad(0)
+            for step in range(-1, TOKENS - 1):
+                if (step + 1) % QUAD == 0 and step + 1 + QUAD < TOKENS:
+                    prepare_text_quad((step + 1) // QUAD + 1)
+                pipeline_step(step)
+
+        with tc.manual_schedule():
+            for step in range(TOKENS - 1, FIRST_STEPS - 1):
+                pipeline_step(step)
+
+        with tc.tile_pool(name="finish", bufs=2) as finish:
+            for step in range(FIRST_STEPS - 1, STEPS + DRAIN):
+                pipeline_step(step)
+
+            def divide_sums(first_col, last_col):
+                weights = sums[:, 0, first_col:last_col]
+                products = sums[:, 1, first_col:last_col]
+                nc.scalar.activation(out=weights, in_=weights, func=FN.Ln)
+                nc.scalar.activation(out=weights, in_=weights, func=FN.Exp, scale=-1.0)
+                nc.gpsimd.tensor_tensor(out=products, in0=products, in1=weights, op=ALU.mult)
+
+            def turned_back(first_col):
+                bank = psum.tile([P, BLOCKS * P], F32, tag="first", name="turned_back")
+                for k in range(BLOCKS):
+                    block = sums[:, 1, first_col + k * P : first_col + (k + 1) * P]
+                    nc.tensor.transpose(bank[:, k * P : (k + 1) * P], block, ident_f32[:])
+                return bank
+
+            def pooled_mean(values, count, result):
+                shape = [P, count, GROUP_VIDEOS]
+                top = finish.tile([P, GROUP_VIDEOS], F32, tag="top", name="top")
+                nc.vector.tensor_reduce(
+                    out=top[:], in_=values.rearrange("a n b -> a b n"), axis=INNERMOST, op=ALU.max
+                )
+                dev = finish.tile([P, TOKENS, GROUP_VIDEOS], F32, tag="dev", name="dev")
+                wgt = finish.tile([P, TOKENS, GROUP_VIDEOS], F32, tag="wgt", name="wgt")
+                nc.vector.tensor_tensor(
+                    out=dev[:, 0:count, :],
+                    in0=values,
+                    in1=top[:].unsqueeze(1).to_broadcast(shape),
+                    op=ALU.subtract,
+                )
+                nc.scalar.activation(
+                    out=wgt[:, 0:count, :], in_=dev[:, 0:count, :], func=FN.Exp, scale=TAU
+                )
+                nc.gpsimd.tensor_tensor(
+                    out=dev[:, 0:count, :], in0=dev[:, 0:count, :], in1=wgt[:, 0:count, :], op=ALU.mult
+                )
+                weight_sum = finish.tile([P, GROUP_VIDEOS], F32, tag="weight_sum", name="weight_sum")
+                nc.vector.tensor_reduce(
+                    out=weight_sum[:],
+                    in_=wgt[:, 0:count, :].rearrange("a n b -> a b n"),
+                    axis=INNERMOST,
+                    op=ALU.add,
+                )
+                product_sum = finish.tile(
+                    [P, GROUP_VIDEOS], F32, tag="product_sum", name="product_sum"
+                )
+                nc.vector.tensor_reduce(
+                    out=product_sum[:],
+                    in_=dev[:, 0:count, :].rearrange("a n b -> a b n"),
+                    axis=INNERMOST,
+                    op=ALU.add,
+                )
+                nc.vector.reciprocal(out=weight_sum[:], in_=weight_sum[:])
+                nc.vector.tensor_tensor(
+                    out=product_sum[:], in0=product_sum[:], in1=weight_sum[:], op=ALU.mult
+                )
+                nc.vector.tensor_tensor(out=result, in0=product_sum[:], in1=top[:], op=ALU.add)
+
+            def finish_text_to_video(group):
+                t2v = finish.tile([P, TOKENS, GROUP_VIDEOS], F32, tag="t2v", name="t2v")
+                tokens_of_bank = BLOCKS * QUAD
+                for first in range(0, TOKENS, tokens_of_bank):
+                    bank = turned_back((group * QUADS + first // QUAD) * P)
+                    tokens = slice(first, first + tokens_of_bank)
+                    nc.vector.tensor_tensor(
+                        out=t2v[:, tokens, :],
+                        in0=bank[:].rearrange("a (t b) -> a t b", b=GROUP_VIDEOS),
+                        in1=frame_top[:, group, tokens, :],
+                        op=ALU.add,
+                    )
+                nc.vector.tensor_tensor(
+                    out=t2v[:],
+                    in0=t2v[:],
+                    in1=mask[:].unsqueeze(2).to_broadcast([P, TOKENS, GROUP_VIDEOS]),
+                    op=ALU.mult,
+                )
+                bar = finish.tile([P, TOKENS, GROUP_VIDEOS], F32, tag="bar", name="bar")
+                nc.vector.tensor_scalar(
+                    out=bar[:], in0=t2v[:], scalar1=0.0, scalar2=BARRED,
+                    op0=ALU.is_equal, op1=ALU.mult,
+                )
+                nc.vector.tensor_tensor(out=t2v[:], in0=t2v[:], in1=bar[:], op=ALU.add)
+                videos = slice(group * GROUP_VIDEOS, (group + 1) * GROUP_VIDEOS)
+                pooled_mean(t2v[:], TOKENS, text_to_video[:, videos])
+
+            def finish_video_to_text(group):
+                bank = turned_back(FRAME_SUM_COLS + group * GROUP_COLS)
+                v2t = finish.tile([P, FRAMES, GROUP_VIDEOS], F32, tag="v2t", name="v2t")
+                nc.vector.tensor_tensor(
+                    out=v2t[:].rearrange("a v b -> a (v b)"),
+                    in0=bank[:],
+                    in1=token_top[:, group, :],
+                    op=ALU.add,
+                )
+                videos = slice(group * GROUP_VIDEOS, (group + 1) * GROUP_VIDEOS)
+                pooled_mean(v2t[:], FRAMES, video_to_text[:, videos])
+
+            ready_cols = SUM_COLS - GROUP_COLS
+            divide_sums(0, ready_cols)
+            for group in range(GROUPS):
+                finish_text_to_video(group)
+            for group in range(GROUPS - 1):
+                finish_video_to_text(group)
+            divide_sums(ready_cols, SUM_COLS)
+            finish_video_to_text(GROUPS - 1)
+
+            result = finish.tile([P, P], F32, name="result", bufs=1)
+            nc.vector.tensor_tensor(
+                out=result[:], in0=text_to_video[:], in1=video_to_text[:], op=ALU.add
+            )
+            nc.vector.tensor_scalar_mul(out=result[:], in0=result[:], scalar1=0.5)
+            nc.sync.dma_start(out=out, in_=result[:])

@@ -32,6 +32,7 @@ SUM_COLS = FRAME_SUM_COLS + GROUPS * GROUP_COLS
 
 FIRST_STEPS = GROUPS * TOKENS
 STEPS = FIRST_STEPS + TOKENS
+FIRST_SWEEP_PASSES = 2
 DRAIN = 2
 
 FLOPS = 2 * (P * TOKENS) * (P * FRAMES) * FEATURES
@@ -90,19 +91,20 @@ def tile_mug_head_kernel(tc, text_feat, video_feat, text_mask, out):
                 nc.tensor.transpose(bank[:, j, :], rows[:, j * P : (j + 1) * P], ident_bf16[:])
             return bank
 
-        def similarities(token, group, tag):
+        def similarities(token, group, tag, times):
             sim = psum.tile([P, GROUP_COLS], F32, tag=tag, name="sim")
             texts = slice(token * P, (token + 1) * P)
             cols = slice(group * GROUP_COLS, (group + 1) * GROUP_COLS)
-            nc.tensor.matmul_mx(
-                out=sim[:],
-                lhsT=text_codes[:, texts].bitcast(FP8X4),
-                lhsT_scale=text_scales[:, texts],
-                rhs=video_codes[:, cols].bitcast(FP8X4),
-                rhs_scale=video_scales[:, cols],
-                start=True,
-                stop=True,
-            )
+            for repeat in range(times):
+                nc.tensor.matmul_mx(
+                    out=sim[:],
+                    lhsT=text_codes[:, texts].bitcast(FP8X4),
+                    lhsT_scale=text_scales[:, texts],
+                    rhs=video_codes[:, cols].bitcast(FP8X4),
+                    rhs_scale=video_scales[:, cols],
+                    start=True,
+                    stop=True,
+                )
             return sim
 
         sim_first = {}
@@ -121,9 +123,9 @@ def tile_mug_head_kernel(tc, text_feat, video_feat, text_mask, out):
         def multiply(step):
             token = step % TOKENS
             if in_first_sweep(step):
-                sim_first[step] = similarities(token, step // TOKENS, "first")
+                sim_first[step] = similarities(token, step // TOKENS, "first", FIRST_SWEEP_PASSES)
             if in_second_sweep(step):
-                sim_second[step] = similarities(token, step // TOKENS - 1, "second")
+                sim_second[step] = similarities(token, step // TOKENS - 1, "second", 1)
 
         def subtract_tops(step):
             token = step % TOKENS

@@ -33,7 +33,8 @@ SUM_COLS = FRAME_SUM_COLS + GROUPS * GROUP_COLS
 FIRST_STEPS = GROUPS * TOKENS
 STEPS = FIRST_STEPS + TOKENS
 FIRST_SWEEP_PASSES = 2
-DRAIN = 2
+PAIR = 2
+SUM_LAG = 4
 
 FLOPS = 2 * (P * TOKENS) * (P * FRAMES) * FEATURES
 
@@ -43,8 +44,6 @@ def tile_mug_head_kernel(tc, text_feat, video_feat, text_mask, out):
     with ExitStack() as pools:
         consts = pools.enter_context(tc.tile_pool(name="consts", bufs=1))
         keep = pools.enter_context(tc.tile_pool(name="keep", bufs=1))
-        quad_work = pools.enter_context(tc.tile_pool(name="quad_work", bufs=2))
-        token_work = pools.enter_context(tc.tile_pool(name="token_work", bufs=4))
         psum = pools.enter_context(tc.psum_pool(name="psum", bufs=2))
 
         ident_f32 = consts.tile([P, P], F32, name="ident_f32")
@@ -80,16 +79,72 @@ def tile_mug_head_kernel(tc, text_feat, video_feat, text_mask, out):
                 out=acc, lhsT=block, rhs=ident_f32[:], is_transpose=True, start=start, stop=stop
             )
 
-        def inverse_norm(square_sum, inverse):
-            nc.vector.tensor_scalar_max(out=square_sum, in0=square_sum, scalar1=EPS * EPS)
-            nc.scalar.sqrt(out=inverse, in_=square_sum)
-            nc.vector.reciprocal(out=inverse, in_=inverse)
+        def inverse_norms(pool, raw, count):
+            by_scalar = pool.tile([P, count // 2], F32, name="squares_by_scalar", bufs=1)
+            by_vector = pool.tile([P, count // 2], F32, name="squares_by_vector", bufs=1)
+            for i in range(count):
+                total = slice(i // 2, i // 2 + 1)
+                if i % 2 == 0:
+                    squares = pool.tile([P, FEATURES], BF16, tag="squares_s", name="squares_s")
+                    nc.scalar.activation(
+                        out=squares[:], in_=raw[:, i, :], func=FN.Square, accum_out=by_scalar[:, total]
+                    )
+                else:
+                    squares = pool.tile([P, FEATURES], F32, tag="squares_v", name="squares_v")
+                    nc.vector.scalar_tensor_tensor(
+                        out=squares[:], in0=raw[:, i, :], scalar=1.0, in1=raw[:, i, :],
+                        op0=ALU.mult, op1=ALU.mult, accum_out=by_vector[:, total],
+                    )
+            inverse = pool.tile([P, 2, count // 2], F32, name="inverse", bufs=1)
+            for parity, square_sum in enumerate((by_scalar, by_vector)):
+                nc.vector.tensor_scalar_max(out=square_sum[:], in0=square_sum[:], scalar1=EPS * EPS)
+                nc.scalar.sqrt(out=inverse[:, parity, :], in_=square_sum[:])
+                nc.vector.reciprocal(out=inverse[:, parity, :], in_=inverse[:, parity, :])
+            return inverse
 
         def features_to_partitions(rows):
             bank = psum.tile([P, PACK, P], BF16, tag="second", name="turned_rows")
             for j in range(PACK):
                 nc.tensor.transpose(bank[:, j, :], rows[:, j * P : (j + 1) * P], ident_bf16[:])
             return bank
+
+        with tc.tile_pool(name="video_prep", bufs=2) as video_prep:
+            video_raw = video_prep.tile([P, FRAMES, FEATURES], BF16, name="video_raw", bufs=1)
+            for first in range(0, FRAMES, 4):
+                nc.sync.dma_start(
+                    out=video_raw[:, first : first + 4, :], in_=video_feat[:, first : first + 4, :]
+                )
+            warm = video_prep.tile([P, 1], F32, name="warm", bufs=1)
+            nc.vector.memset(warm[:], 1.0)
+            nc.scalar.sqrt(out=warm[:], in_=warm[:])
+            video_inverse = inverse_norms(video_prep, video_raw, FRAMES)
+            video_grouped = video_prep.tile(
+                [P, GROUPS, FRAMES, GROUP_VIDEOS, PACK], BF16,
+                name="video_grouped", bufs=1, align_bytes=64,
+            )
+            for v in range(FRAMES):
+                rows = video_prep.tile([P, FEATURES], BF16, tag="rows", name="rows", bufs=3)
+                nc.vector.tensor_scalar_mul(
+                    out=rows[:],
+                    in0=video_raw[:, v, :],
+                    scalar1=video_inverse[:, v % 2, v // 2 : v // 2 + 1],
+                )
+                bank = features_to_partitions(rows)
+                copy = nc.scalar.copy if v % 2 == 0 else nc.vector.tensor_copy
+                copy(
+                    out=video_grouped[:, :, v, :, :],
+                    in_=bank[:].rearrange("p j (g b) -> p g b j", g=GROUPS),
+                )
+            for group in range(GROUPS):
+                cols = slice(group * GROUP_COLS, (group + 1) * GROUP_COLS)
+                nc.vector.quantize_mx(
+                    out=video_codes[:, cols].bitcast(FP8X4),
+                    scales=video_scales[:, cols],
+                    in_=video_grouped[:, group, :, :, :].rearrange("p v b j -> p (v b j)"),
+                )
+
+        quad_work = pools.enter_context(tc.tile_pool(name="quad_work", bufs=3))
+        pair_work = pools.enter_context(tc.tile_pool(name="pair_work", bufs=3))
 
         def similarities(token, group, tag, times):
             sim = psum.tile([P, GROUP_COLS], F32, tag=tag, name="sim")
@@ -129,20 +184,32 @@ def tile_mug_head_kernel(tc, text_feat, video_feat, text_mask, out):
 
         def subtract_tops(step):
             token = step % TOKENS
+            group = step // TOKENS
+            top_f = None
+            if in_first_sweep(step):
+                top_f = frame_top[:, group, token, :]
+                nc.vector.tensor_reduce(
+                    out=top_f,
+                    in_=sim_first[step][:].rearrange("a (v b) -> a b v", v=FRAMES),
+                    axis=INNERMOST,
+                    op=ALU.max,
+                )
             if in_second_sweep(step):
-                dev_t = token_work.tile([P, GROUP_COLS], F32, tag="dev_t", name="dev_t")
-                wgt_t = token_work.tile([P, GROUP_COLS], F32, tag="wgt_t", name="wgt_t")
-                token_tiles[step] = (dev_t, wgt_t)
+                if step % PAIR == 0:
+                    pair_shape = [P, PAIR, GROUP_COLS]
+                    token_tiles[step // PAIR] = (
+                        pair_work.tile(pair_shape, F32, tag="dev_t", name="dev_t"),
+                        pair_work.tile(pair_shape, F32, tag="wgt_t", name="wgt_t"),
+                    )
                 nc.vector.scalar_tensor_tensor(
-                    out=dev_t[:],
+                    out=token_tiles[step // PAIR][0][:, step % PAIR, :],
                     in0=sim_second[step][:],
                     scalar=mask[:, token : token + 1],
-                    in1=token_top[:, step // TOKENS - 1, :],
+                    in1=token_top[:, group - 1, :],
                     op0=ALU.mult,
                     op1=ALU.subtract,
                 )
             if in_first_sweep(step):
-                group = step // TOKENS
                 sim = sim_first[step]
                 if step % QUAD == 0:
                     quad_shape = [P, FRAMES, QUAD, GROUP_VIDEOS]
@@ -150,16 +217,8 @@ def tile_mug_head_kernel(tc, text_feat, video_feat, text_mask, out):
                         quad_work.tile(quad_shape, F32, tag="dev_f", name="dev_f"),
                         quad_work.tile(quad_shape, F32, tag="wgt_f", name="wgt_f"),
                     )
-                dev_f = frame_tiles[step // QUAD][0]
-                top_f = frame_top[:, group, token, :]
-                nc.vector.tensor_reduce(
-                    out=top_f,
-                    in_=sim[:].rearrange("a (v b) -> a b v", v=FRAMES),
-                    axis=INNERMOST,
-                    op=ALU.max,
-                )
                 nc.vector.tensor_tensor(
-                    out=dev_f[:, :, step % QUAD, :],
+                    out=frame_tiles[step // QUAD][0][:, :, step % QUAD, :],
                     in0=sim[:].rearrange("a (v b) -> a v b", v=FRAMES),
                     in1=top_f.unsqueeze(1).to_broadcast([P, FRAMES, GROUP_VIDEOS]),
                     op=ALU.subtract,
@@ -180,10 +239,10 @@ def tile_mug_head_kernel(tc, text_feat, video_feat, text_mask, out):
         def weigh(step):
             token = step % TOKENS
             if in_second_sweep(step):
-                dev_t, wgt_t = token_tiles[step]
+                dev_t, wgt_t = token_tiles[step // PAIR]
                 nc.scalar.activation(
-                    out=wgt_t[:],
-                    in_=dev_t[:],
+                    out=wgt_t[:, step % PAIR, :],
+                    in_=dev_t[:, step % PAIR, :],
                     func=FN.Exp,
                     scale=TAU,
                     bias=barred[:, token : token + 1],
@@ -198,16 +257,18 @@ def tile_mug_head_kernel(tc, text_feat, video_feat, text_mask, out):
                 )
 
         def form_products(step):
+            if step % PAIR != PAIR - 1:
+                return
             if in_second_sweep(step):
-                dev_t, wgt_t = token_tiles[step]
+                dev_t, wgt_t = token_tiles[step // PAIR]
                 nc.gpsimd.tensor_tensor(out=dev_t[:], in0=dev_t[:], in1=wgt_t[:], op=ALU.mult)
             if in_first_sweep(step):
                 dev_f, wgt_f = frame_tiles[step // QUAD]
-                slot = step % QUAD
+                slots = slice(step % QUAD - (PAIR - 1), step % QUAD + 1)
                 nc.gpsimd.tensor_tensor(
-                    out=dev_f[:, :, slot, :],
-                    in0=dev_f[:, :, slot, :],
-                    in1=wgt_f[:, :, slot, :],
+                    out=dev_f[:, :, slots, :],
+                    in0=dev_f[:, :, slots, :],
+                    in1=wgt_f[:, :, slots, :],
                     op=ALU.mult,
                 )
 
@@ -221,19 +282,19 @@ def tile_mug_head_kernel(tc, text_feat, video_feat, text_mask, out):
                     psum.tile([P, GROUP_COLS], F32, tag="weight_sums", name="weight_sums", bufs=1),
                     psum.tile([P, GROUP_COLS], F32, tag="product_sums", name="product_sums", bufs=1),
                 )
-            dev_t, wgt_t = token_tiles[step]
-            for acc, terms in zip(group_banks[group], (wgt_t, dev_t)):
+            dev_t, wgt_t = token_tiles[step // PAIR]
+            for plane, terms in enumerate((wgt_t, dev_t)):
+                acc = group_banks[group][plane]
                 for k in range(BLOCKS):
                     cols = slice(k * P, (k + 1) * P)
                     transpose_add(
                         acc[:, cols],
-                        terms[:, cols],
+                        terms[:, step % PAIR, cols],
                         token == 0 and k == 0,
                         token == TOKENS - 1 and k == BLOCKS - 1,
                     )
-            if token == TOKENS - 1:
-                first_col = FRAME_SUM_COLS + group * GROUP_COLS
-                for plane, acc in enumerate(group_banks[group]):
+                if token == TOKENS - 1:
+                    first_col = FRAME_SUM_COLS + group * GROUP_COLS
                     nc.scalar.copy(out=sums[:, plane, first_col : first_col + GROUP_COLS], in_=acc[:])
 
         def add_up_frames(step):
@@ -263,88 +324,30 @@ def tile_mug_head_kernel(tc, text_feat, video_feat, text_mask, out):
             subtract_tops(step)
             weigh(step)
             form_products(step - 1)
-            add_up_tokens(step - 2)
-            add_up_frames(step - QUAD)
-            store_frame_sums(step - QUAD - 1)
+            add_up_tokens(step - SUM_LAG)
+            add_up_frames(step - SUM_LAG)
+            store_frame_sums(step - SUM_LAG - 1)
 
-        with tc.tile_pool(name="prep", bufs=2) as prep:
-            video_raw = prep.tile([P, FRAMES, FEATURES], BF16, name="video_raw", bufs=1)
-            nc.sync.dma_start(out=video_raw[:], in_=video_feat)
-            text_raw = prep.tile([P, TOKENS, FEATURES], BF16, name="text_raw", bufs=1)
+        with tc.tile_pool(name="text_prep", bufs=2) as text_prep:
+            text_raw = text_prep.tile([P, TOKENS, FEATURES], BF16, name="text_raw", bufs=1)
             for first in range(0, TOKENS, 8):
                 nc.sync.dma_start(
                     out=text_raw[:, first : first + 8, :], in_=text_feat[:, first : first + 8, :]
                 )
-
-            warm = prep.tile([P, 1], F32, name="warm", bufs=1)
-            nc.vector.memset(warm[:], 1.0)
-            nc.scalar.sqrt(out=warm[:], in_=warm[:])
-
-            def square_sum_on_scalar(rows, total):
-                squares = prep.tile([P, FEATURES], BF16, tag="squares_s", name="squares_s")
-                nc.scalar.activation(out=squares[:], in_=rows, func=FN.Square, accum_out=total)
-
-            def square_sum_on_vector(rows, total):
-                squares = prep.tile([P, FEATURES], F32, tag="squares_v", name="squares_v")
-                nc.vector.scalar_tensor_tensor(
-                    out=squares[:], in0=rows, scalar=1.0, in1=rows,
-                    op0=ALU.mult, op1=ALU.mult, accum_out=total,
-                )
-
-            half = TOKENS // 2
-            video_squares = prep.tile([P, FRAMES], F32, name="video_squares", bufs=1)
-            text_squares_s = prep.tile([P, half], F32, name="text_squares_s", bufs=1)
-            text_squares_v = prep.tile([P, half], F32, name="text_squares_v", bufs=1)
-            video_inverse = prep.tile([P, FRAMES], F32, name="video_inverse", bufs=1)
-            text_inverse = prep.tile([P, TOKENS], F32, name="text_inverse", bufs=1)
-
-            for v in range(FRAMES):
-                square_sum_on_scalar(video_raw[:, v, :], video_squares[:, v : v + 1])
-            inverse_norm(video_squares[:], video_inverse[:])
-
-            video_grouped = prep.tile(
-                [P, GROUPS, FRAMES, GROUP_VIDEOS, PACK], BF16,
-                name="video_grouped", bufs=1, align_bytes=64,
-            )
-            for v in range(FRAMES):
-                rows = prep.tile([P, FEATURES], BF16, tag="rows", name="rows", bufs=3)
-                nc.vector.tensor_scalar_mul(
-                    out=rows[:], in0=video_raw[:, v, :], scalar1=video_inverse[:, v : v + 1]
-                )
-                bank = features_to_partitions(rows)
-                copy = nc.scalar.copy if v % 2 == 0 else nc.vector.tensor_copy
-                copy(
-                    out=video_grouped[:, :, v, :, :],
-                    in_=bank[:].rearrange("p j (g b) -> p g b j", g=GROUPS),
-                )
-            for group in range(GROUPS):
-                cols = slice(group * GROUP_COLS, (group + 1) * GROUP_COLS)
-                nc.vector.quantize_mx(
-                    out=video_codes[:, cols].bitcast(FP8X4),
-                    scales=video_scales[:, cols],
-                    in_=video_grouped[:, group, :, :, :].rearrange("p v b j -> p (v b j)"),
-                )
-
-            for token in range(half):
-                square_sum_on_scalar(text_raw[:, token, :], text_squares_s[:, token : token + 1])
-                square_sum_on_vector(
-                    text_raw[:, half + token, :], text_squares_v[:, token : token + 1]
-                )
-            inverse_norm(text_squares_s[:], text_inverse[:, 0:half])
-            inverse_norm(text_squares_v[:], text_inverse[:, half:TOKENS])
+            text_inverse = inverse_norms(text_prep, text_raw, TOKENS)
 
             def prepare_text_quad(quad):
-                grouped = prep.tile(
+                grouped = text_prep.tile(
                     [P, QUAD, P, PACK], BF16, tag="text_grouped", name="text_grouped", align_bytes=64
                 )
                 for slot in range(QUAD):
                     token = quad * QUAD + slot
-                    rows = prep.tile([P, FEATURES], BF16, tag="rows", name="rows", bufs=3)
+                    rows = text_prep.tile([P, FEATURES], BF16, tag="rows", name="rows", bufs=3)
                     nc.scalar.activation(
                         out=rows[:],
                         in_=text_raw[:, token, :],
                         func=FN.Copy,
-                        scale=text_inverse[:, token : token + 1],
+                        scale=text_inverse[:, token % 2, token // 2 : token // 2 + 1],
                     )
                     bank = features_to_partitions(rows)
                     nc.scalar.copy(
@@ -368,7 +371,7 @@ def tile_mug_head_kernel(tc, text_feat, video_feat, text_mask, out):
                 pipeline_step(step)
 
         with tc.tile_pool(name="finish", bufs=2) as finish:
-            for step in range(FIRST_STEPS - 1, STEPS + DRAIN):
+            for step in range(FIRST_STEPS - 1, STEPS + SUM_LAG + 1):
                 pipeline_step(step)
 
             def divide_sums(first_col, last_col):
@@ -386,41 +389,22 @@ def tile_mug_head_kernel(tc, text_feat, video_feat, text_mask, out):
                 return bank
 
             def pooled_mean(values, count, result):
-                shape = [P, count, GROUP_VIDEOS]
+                shape = [P, GROUP_VIDEOS, count]
                 top = finish.tile([P, GROUP_VIDEOS], F32, tag="top", name="top")
-                nc.vector.tensor_reduce(
-                    out=top[:], in_=values.rearrange("a n b -> a b n"), axis=INNERMOST, op=ALU.max
-                )
-                dev = finish.tile([P, TOKENS, GROUP_VIDEOS], F32, tag="dev", name="dev")
-                wgt = finish.tile([P, TOKENS, GROUP_VIDEOS], F32, tag="wgt", name="wgt")
+                nc.vector.tensor_reduce(out=top[:], in_=values, axis=INNERMOST, op=ALU.max)
+                dev = finish.tile(shape, F32, tag="dev%d" % count, name="dev")
+                wgt = finish.tile(shape, F32, tag="wgt%d" % count, name="wgt")
                 nc.vector.tensor_tensor(
-                    out=dev[:, 0:count, :],
-                    in0=values,
-                    in1=top[:].unsqueeze(1).to_broadcast(shape),
-                    op=ALU.subtract,
+                    out=dev[:], in0=values, in1=top[:].unsqueeze(2).to_broadcast(shape), op=ALU.subtract
                 )
-                nc.scalar.activation(
-                    out=wgt[:, 0:count, :], in_=dev[:, 0:count, :], func=FN.Exp, scale=TAU
-                )
-                nc.gpsimd.tensor_tensor(
-                    out=dev[:, 0:count, :], in0=dev[:, 0:count, :], in1=wgt[:, 0:count, :], op=ALU.mult
-                )
+                nc.scalar.activation(out=wgt[:], in_=dev[:], func=FN.Exp, scale=TAU)
+                nc.gpsimd.tensor_tensor(out=dev[:], in0=dev[:], in1=wgt[:], op=ALU.mult)
                 weight_sum = finish.tile([P, GROUP_VIDEOS], F32, tag="weight_sum", name="weight_sum")
-                nc.vector.tensor_reduce(
-                    out=weight_sum[:],
-                    in_=wgt[:, 0:count, :].rearrange("a n b -> a b n"),
-                    axis=INNERMOST,
-                    op=ALU.add,
-                )
+                nc.vector.tensor_reduce(out=weight_sum[:], in_=wgt[:], axis=INNERMOST, op=ALU.add)
                 product_sum = finish.tile(
                     [P, GROUP_VIDEOS], F32, tag="product_sum", name="product_sum"
                 )
-                nc.vector.tensor_reduce(
-                    out=product_sum[:],
-                    in_=dev[:, 0:count, :].rearrange("a n b -> a b n"),
-                    axis=INNERMOST,
-                    op=ALU.add,
-                )
+                nc.vector.tensor_reduce(out=product_sum[:], in_=dev[:], axis=INNERMOST, op=ALU.add)
                 nc.vector.reciprocal(out=weight_sum[:], in_=weight_sum[:])
                 nc.vector.tensor_tensor(
                     out=product_sum[:], in0=product_sum[:], in1=weight_sum[:], op=ALU.mult
@@ -428,24 +412,22 @@ def tile_mug_head_kernel(tc, text_feat, video_feat, text_mask, out):
                 nc.vector.tensor_tensor(out=result, in0=product_sum[:], in1=top[:], op=ALU.add)
 
             def finish_text_to_video(group):
-                t2v = finish.tile([P, TOKENS, GROUP_VIDEOS], F32, tag="t2v", name="t2v")
+                shape = [P, GROUP_VIDEOS, TOKENS]
+                t2v = finish.tile(shape, F32, tag="t2v", name="t2v")
                 tokens_of_bank = BLOCKS * QUAD
                 for first in range(0, TOKENS, tokens_of_bank):
                     bank = turned_back((group * QUADS + first // QUAD) * P)
                     tokens = slice(first, first + tokens_of_bank)
                     nc.vector.tensor_tensor(
-                        out=t2v[:, tokens, :],
-                        in0=bank[:].rearrange("a (t b) -> a t b", b=GROUP_VIDEOS),
-                        in1=frame_top[:, group, tokens, :],
+                        out=t2v[:, :, tokens],
+                        in0=bank[:].rearrange("a (t b) -> a b t", b=GROUP_VIDEOS),
+                        in1=frame_top[:, group, tokens, :].rearrange("a t b -> a b t"),
                         op=ALU.add,
                     )
                 nc.vector.tensor_tensor(
-                    out=t2v[:],
-                    in0=t2v[:],
-                    in1=mask[:].unsqueeze(2).to_broadcast([P, TOKENS, GROUP_VIDEOS]),
-                    op=ALU.mult,
+                    out=t2v[:], in0=t2v[:], in1=mask[:].unsqueeze(1).to_broadcast(shape), op=ALU.mult
                 )
-                bar = finish.tile([P, TOKENS, GROUP_VIDEOS], F32, tag="bar", name="bar")
+                bar = finish.tile(shape, F32, tag="bar", name="bar")
                 nc.vector.tensor_scalar(
                     out=bar[:], in0=t2v[:], scalar1=0.0, scalar2=BARRED,
                     op0=ALU.is_equal, op1=ALU.mult,
@@ -456,11 +438,11 @@ def tile_mug_head_kernel(tc, text_feat, video_feat, text_mask, out):
 
             def finish_video_to_text(group):
                 bank = turned_back(FRAME_SUM_COLS + group * GROUP_COLS)
-                v2t = finish.tile([P, FRAMES, GROUP_VIDEOS], F32, tag="v2t", name="v2t")
+                v2t = finish.tile([P, GROUP_VIDEOS, FRAMES], F32, tag="v2t", name="v2t")
                 nc.vector.tensor_tensor(
-                    out=v2t[:].rearrange("a v b -> a (v b)"),
-                    in0=bank[:],
-                    in1=token_top[:, group, :],
+                    out=v2t[:],
+                    in0=bank[:].rearrange("a (v b) -> a b v", v=FRAMES),
+                    in1=token_top[:, group, :].rearrange("a (v b) -> a b v", v=FRAMES),
                     op=ALU.add,
                 )
                 videos = slice(group * GROUP_VIDEOS, (group + 1) * GROUP_VIDEOS)

@@ -27,8 +27,9 @@ GROUP_COLS = FRAMES * GROUP_VIDEOS
 BLOCKS = GROUP_COLS // P
 QUAD = 4
 QUADS = TOKENS // QUAD
-FRAME_SUM_COLS = GROUPS * QUADS * P
-SUM_COLS = FRAME_SUM_COLS + GROUPS * GROUP_COLS
+FRAME_SUM_COLS = QUADS * P
+PHASE_SUM_COLS = GROUP_COLS + FRAME_SUM_COLS
+SUM_COLS = GROUPS * PHASE_SUM_COLS
 
 FIRST_STEPS = GROUPS * TOKENS
 STEPS = FIRST_STEPS + TOKENS
@@ -169,6 +170,12 @@ def tile_mug_head_kernel(tc, text_feat, video_feat, text_mask, out):
         quad_banks = {}
         group_banks = {}
 
+        def frame_sum_col(group):
+            return group * PHASE_SUM_COLS
+
+        def token_sum_col(group):
+            return (group + 1) * PHASE_SUM_COLS - GROUP_COLS
+
         def in_first_sweep(step):
             return 0 <= step < FIRST_STEPS
 
@@ -294,7 +301,7 @@ def tile_mug_head_kernel(tc, text_feat, video_feat, text_mask, out):
                         token == TOKENS - 1 and k == BLOCKS - 1,
                     )
                 if token == TOKENS - 1:
-                    first_col = FRAME_SUM_COLS + group * GROUP_COLS
+                    first_col = token_sum_col(group)
                     nc.scalar.copy(out=sums[:, plane, first_col : first_col + GROUP_COLS], in_=acc[:])
 
         def add_up_frames(step):
@@ -304,7 +311,7 @@ def tile_mug_head_kernel(tc, text_feat, video_feat, text_mask, out):
             plane = (step % QUAD) // 2
             first_frame = (step % 2) * (FRAMES // 2)
             if step % QUAD == 0:
-                quad_banks[quad] = psum.tile([P, 2, P], F32, tag="quad_sums", name="quad_sums")
+                quad_banks[quad] = psum.tile([P, 2, P], F32, tag="quad_sums", name="quad_sums", bufs=1)
             terms = frame_tiles[quad][1 - plane]
             for v in range(first_frame, first_frame + FRAMES // 2):
                 transpose_add(
@@ -316,17 +323,19 @@ def tile_mug_head_kernel(tc, text_feat, video_feat, text_mask, out):
 
         def store_frame_sums(step):
             if in_first_sweep(step) and step % QUAD == QUAD - 1:
-                quad = step // QUAD
-                nc.scalar.copy(out=sums[:, :, quad * P : (quad + 1) * P], in_=quad_banks[quad][:])
+                first_col = frame_sum_col(step // TOKENS) + (step % TOKENS) // QUAD * P
+                nc.scalar.copy(
+                    out=sums[:, :, first_col : first_col + P], in_=quad_banks[step // QUAD][:]
+                )
 
         def pipeline_step(step):
             multiply(step + 1)
+            store_frame_sums(step - SUM_LAG - 1)
             subtract_tops(step)
             weigh(step)
             form_products(step - 1)
             add_up_tokens(step - SUM_LAG)
             add_up_frames(step - SUM_LAG)
-            store_frame_sums(step - SUM_LAG - 1)
 
         with tc.tile_pool(name="text_prep", bufs=2) as text_prep:
             text_raw = text_prep.tile([P, TOKENS, FEATURES], BF16, name="text_raw", bufs=1)
@@ -366,100 +375,169 @@ def tile_mug_head_kernel(tc, text_feat, video_feat, text_mask, out):
                     prepare_text_quad((step + 1) // QUAD + 1)
                 pipeline_step(step)
 
-        with tc.manual_schedule():
-            for step in range(TOKENS - 1, FIRST_STEPS - 1):
-                pipeline_step(step)
+        finish = pools.enter_context(tc.tile_pool(name="finish", bufs=2))
 
-        with tc.tile_pool(name="finish", bufs=2) as finish:
-            for step in range(FIRST_STEPS - 1, STEPS + SUM_LAG + 1):
-                pipeline_step(step)
+        def turn_back(made, first_col):
+            made["bank"] = psum.tile([P, BLOCKS * P], F32, tag="back", name="turned_back", bufs=1)
+            for k in range(BLOCKS):
+                block = sums[:, 1, first_col + k * P : first_col + (k + 1) * P]
+                nc.tensor.transpose(made["bank"][:, k * P : (k + 1) * P], block, ident_f32[:])
 
-            def divide_sums(first_col, last_col):
-                weights = sums[:, 0, first_col:last_col]
-                products = sums[:, 1, first_col:last_col]
+        def division_pieces(phase):
+            first_col = token_sum_col(phase - 1) if phase > 0 else 0
+            last_col = frame_sum_col(phase) + FRAME_SUM_COLS if phase < GROUPS else SUM_COLS
+            weights = sums[:, 0, first_col:last_col]
+
+            def invert():
                 nc.scalar.activation(out=weights, in_=weights, func=FN.Ln)
                 nc.scalar.activation(out=weights, in_=weights, func=FN.Exp, scale=-1.0)
-                nc.gpsimd.tensor_tensor(out=products, in0=products, in1=weights, op=ALU.mult)
 
-            def turned_back(first_col):
-                bank = psum.tile([P, BLOCKS * P], F32, tag="first", name="turned_back")
-                for k in range(BLOCKS):
-                    block = sums[:, 1, first_col + k * P : first_col + (k + 1) * P]
-                    nc.tensor.transpose(bank[:, k * P : (k + 1) * P], block, ident_f32[:])
-                return bank
+            def multiply_by_inverse(col):
+                cols = slice(col, col + GROUP_COLS)
+                nc.gpsimd.tensor_tensor(
+                    out=sums[:, 1, cols], in0=sums[:, 1, cols], in1=sums[:, 0, cols], op=ALU.mult
+                )
 
-            def pooled_mean(values, count, result):
-                shape = [P, GROUP_VIDEOS, count]
-                top = finish.tile([P, GROUP_VIDEOS], F32, tag="top", name="top")
-                nc.vector.tensor_reduce(out=top[:], in_=values, axis=INNERMOST, op=ALU.max)
-                dev = finish.tile(shape, F32, tag="dev%d" % count, name="dev")
-                wgt = finish.tile(shape, F32, tag="wgt%d" % count, name="wgt")
+            pieces = [invert]
+            for col in range(first_col, last_col, GROUP_COLS):
+                pieces.append(lambda col=col: multiply_by_inverse(col))
+            return pieces
+
+        def pooled_mean_pieces(made, count, result):
+            shape = [P, GROUP_VIDEOS, count]
+            small = [P, GROUP_VIDEOS]
+
+            def find_top():
+                made["top"] = finish.tile(small, F32, tag="top", name="top")
+                nc.vector.tensor_reduce(
+                    out=made["top"][:], in_=made["values"][:], axis=INNERMOST, op=ALU.max
+                )
+
+            def weigh_deviations():
+                made["dev"] = finish.tile(shape, F32, tag="dev%d" % count, name="dev")
+                made["wgt"] = finish.tile(shape, F32, tag="wgt%d" % count, name="wgt")
                 nc.vector.tensor_tensor(
-                    out=dev[:], in0=values, in1=top[:].unsqueeze(2).to_broadcast(shape), op=ALU.subtract
+                    out=made["dev"][:],
+                    in0=made["values"][:],
+                    in1=made["top"][:].unsqueeze(2).to_broadcast(shape),
+                    op=ALU.subtract,
                 )
-                nc.scalar.activation(out=wgt[:], in_=dev[:], func=FN.Exp, scale=TAU)
-                nc.gpsimd.tensor_tensor(out=dev[:], in0=dev[:], in1=wgt[:], op=ALU.mult)
-                weight_sum = finish.tile([P, GROUP_VIDEOS], F32, tag="weight_sum", name="weight_sum")
-                nc.vector.tensor_reduce(out=weight_sum[:], in_=wgt[:], axis=INNERMOST, op=ALU.add)
-                product_sum = finish.tile(
-                    [P, GROUP_VIDEOS], F32, tag="product_sum", name="product_sum"
+                nc.scalar.activation(out=made["wgt"][:], in_=made["dev"][:], func=FN.Exp, scale=TAU)
+
+            def form_product():
+                nc.gpsimd.tensor_tensor(
+                    out=made["dev"][:], in0=made["dev"][:], in1=made["wgt"][:], op=ALU.mult
                 )
-                nc.vector.tensor_reduce(out=product_sum[:], in_=dev[:], axis=INNERMOST, op=ALU.add)
+
+            def add_weights():
+                made["weight_sum"] = finish.tile(small, F32, tag="weight_sum", name="weight_sum")
+                nc.vector.tensor_reduce(
+                    out=made["weight_sum"][:], in_=made["wgt"][:], axis=INNERMOST, op=ALU.add
+                )
+
+            def add_products():
+                made["product_sum"] = finish.tile(small, F32, tag="product_sum", name="product_sum")
+                nc.vector.tensor_reduce(
+                    out=made["product_sum"][:], in_=made["dev"][:], axis=INNERMOST, op=ALU.add
+                )
+
+            def divide_and_shift():
+                weight_sum = made["weight_sum"]
+                product_sum = made["product_sum"]
                 nc.vector.reciprocal(out=weight_sum[:], in_=weight_sum[:])
                 nc.vector.tensor_tensor(
                     out=product_sum[:], in0=product_sum[:], in1=weight_sum[:], op=ALU.mult
                 )
-                nc.vector.tensor_tensor(out=result, in0=product_sum[:], in1=top[:], op=ALU.add)
-
-            def finish_text_to_video(group):
-                shape = [P, GROUP_VIDEOS, TOKENS]
-                t2v = finish.tile(shape, F32, tag="t2v", name="t2v")
-                tokens_of_bank = BLOCKS * QUAD
-                for first in range(0, TOKENS, tokens_of_bank):
-                    bank = turned_back((group * QUADS + first // QUAD) * P)
-                    tokens = slice(first, first + tokens_of_bank)
-                    nc.vector.tensor_tensor(
-                        out=t2v[:, :, tokens],
-                        in0=bank[:].rearrange("a (t b) -> a b t", b=GROUP_VIDEOS),
-                        in1=frame_top[:, group, tokens, :].rearrange("a t b -> a b t"),
-                        op=ALU.add,
-                    )
                 nc.vector.tensor_tensor(
-                    out=t2v[:], in0=t2v[:], in1=mask[:].unsqueeze(1).to_broadcast(shape), op=ALU.mult
+                    out=result, in0=product_sum[:], in1=made["top"][:], op=ALU.add
                 )
-                bar = finish.tile(shape, F32, tag="bar", name="bar")
+
+            return [
+                find_top, weigh_deviations, form_product, add_weights, add_products, divide_and_shift
+            ]
+
+        def text_to_video_pieces(group):
+            made = {}
+            shape = [P, GROUP_VIDEOS, TOKENS]
+            tokens_of_bank = BLOCKS * QUAD
+
+            def add_frame_top(first):
+                if first == 0:
+                    made["values"] = finish.tile(shape, F32, tag="t2v", name="t2v")
+                tokens = slice(first, first + tokens_of_bank)
+                nc.vector.tensor_tensor(
+                    out=made["values"][:, :, tokens],
+                    in0=made["bank"][:].rearrange("a (t b) -> a b t", b=GROUP_VIDEOS),
+                    in1=frame_top[:, group, tokens, :].rearrange("a t b -> a b t"),
+                    op=ALU.add,
+                )
+
+            def apply_mask():
+                nc.vector.tensor_tensor(
+                    out=made["values"][:],
+                    in0=made["values"][:],
+                    in1=mask[:].unsqueeze(1).to_broadcast(shape),
+                    op=ALU.mult,
+                )
+
+            def find_zeros():
+                made["bar"] = finish.tile(shape, F32, tag="bar", name="bar")
                 nc.vector.tensor_scalar(
-                    out=bar[:], in0=t2v[:], scalar1=0.0, scalar2=BARRED,
+                    out=made["bar"][:], in0=made["values"][:], scalar1=0.0, scalar2=BARRED,
                     op0=ALU.is_equal, op1=ALU.mult,
                 )
-                nc.vector.tensor_tensor(out=t2v[:], in0=t2v[:], in1=bar[:], op=ALU.add)
-                videos = slice(group * GROUP_VIDEOS, (group + 1) * GROUP_VIDEOS)
-                pooled_mean(t2v[:], TOKENS, text_to_video[:, videos])
 
-            def finish_video_to_text(group):
-                bank = turned_back(FRAME_SUM_COLS + group * GROUP_COLS)
-                v2t = finish.tile([P, GROUP_VIDEOS, FRAMES], F32, tag="v2t", name="v2t")
+            def bar_zeros():
                 nc.vector.tensor_tensor(
-                    out=v2t[:],
-                    in0=bank[:].rearrange("a (v b) -> a b v", v=FRAMES),
+                    out=made["values"][:], in0=made["values"][:], in1=made["bar"][:], op=ALU.add
+                )
+
+            pieces = []
+            for first in range(0, TOKENS, tokens_of_bank):
+                first_col = frame_sum_col(group) + first // QUAD * P
+                pieces.append(lambda first_col=first_col: turn_back(made, first_col))
+                pieces.append(lambda first=first: add_frame_top(first))
+            pieces.extend([apply_mask, find_zeros, bar_zeros])
+            videos = slice(group * GROUP_VIDEOS, (group + 1) * GROUP_VIDEOS)
+            pieces.extend(pooled_mean_pieces(made, TOKENS, text_to_video[:, videos]))
+            return pieces
+
+        def video_to_text_pieces(group):
+            made = {}
+
+            def add_token_top():
+                made["values"] = finish.tile([P, GROUP_VIDEOS, FRAMES], F32, tag="v2t", name="v2t")
+                nc.vector.tensor_tensor(
+                    out=made["values"][:],
+                    in0=made["bank"][:].rearrange("a (v b) -> a b v", v=FRAMES),
                     in1=token_top[:, group, :].rearrange("a (v b) -> a b v", v=FRAMES),
                     op=ALU.add,
                 )
-                videos = slice(group * GROUP_VIDEOS, (group + 1) * GROUP_VIDEOS)
-                pooled_mean(v2t[:], FRAMES, video_to_text[:, videos])
 
-            ready_cols = SUM_COLS - GROUP_COLS
-            divide_sums(0, ready_cols)
-            for group in range(GROUPS):
-                finish_text_to_video(group)
-            for group in range(GROUPS - 1):
-                finish_video_to_text(group)
-            divide_sums(ready_cols, SUM_COLS)
-            finish_video_to_text(GROUPS - 1)
+            pieces = [lambda: turn_back(made, token_sum_col(group)), add_token_top]
+            videos = slice(group * GROUP_VIDEOS, (group + 1) * GROUP_VIDEOS)
+            pieces.extend(pooled_mean_pieces(made, FRAMES, video_to_text[:, videos]))
+            return pieces
 
-            result = finish.tile([P, P], F32, name="result", bufs=1)
-            nc.vector.tensor_tensor(
-                out=result[:], in0=text_to_video[:], in1=video_to_text[:], op=ALU.add
-            )
-            nc.vector.tensor_scalar_mul(out=result[:], in0=result[:], scalar1=0.5)
-            nc.sync.dma_start(out=out, in_=result[:])
+        piece_after = {}
+        for phase in range(GROUPS + 1):
+            pieces = division_pieces(phase)
+            if phase < GROUPS:
+                pieces.extend(text_to_video_pieces(phase))
+            if phase > 0:
+                pieces.extend(video_to_text_pieces(phase - 1))
+            assert len(pieces) <= TOKENS
+            for k, piece in enumerate(pieces):
+                piece_after[(phase + 1) * TOKENS + SUM_LAG + k] = piece
+
+        for step in range(TOKENS - 1, max(piece_after) + 1):
+            pipeline_step(step)
+            if step in piece_after:
+                piece_after[step]()
+
+        result = finish.tile([P, P], F32, name="result", bufs=1)
+        nc.vector.tensor_tensor(
+            out=result[:], in0=text_to_video[:], in1=video_to_text[:], op=ALU.add
+        )
+        nc.vector.tensor_scalar_mul(out=result[:], in0=result[:], scalar1=0.5)
+        nc.sync.dma_start(out=out, in_=result[:])

@@ -36,6 +36,7 @@ STEPS = FIRST_STEPS + TOKENS
 FIRST_SWEEP_PASSES = 2
 PAIR = 2
 SUM_LAG = 4
+PIECES_PER_STEP = 2
 
 FLOPS = 2 * (P * TOKENS) * (P * FRAMES) * FEATURES
 
@@ -72,8 +73,6 @@ def tile_mug_head_kernel(tc, text_feat, video_feat, text_mask, out):
         frame_top = keep.tile([P, GROUPS, TOKENS, GROUP_VIDEOS], F32, name="frame_top")
         token_top = keep.tile([P, GROUPS, GROUP_COLS], F32, name="token_top")
         sums = keep.tile([P, 2, SUM_COLS], F32, name="sums")
-        text_to_video = keep.tile([P, P], F32, name="text_to_video")
-        video_to_text = keep.tile([P, P], F32, name="video_to_text")
 
         def transpose_add(acc, block, start, stop):
             nc.tensor.matmul(
@@ -311,7 +310,7 @@ def tile_mug_head_kernel(tc, text_feat, video_feat, text_mask, out):
             plane = (step % QUAD) // 2
             first_frame = (step % 2) * (FRAMES // 2)
             if step % QUAD == 0:
-                quad_banks[quad] = psum.tile([P, 2, P], F32, tag="quad_sums", name="quad_sums", bufs=1)
+                quad_banks[quad] = psum.tile([P, 2, P], F32, tag="quad_sums", name="quad_sums")
             terms = frame_tiles[quad][1 - plane]
             for v in range(first_frame, first_frame + FRAMES // 2):
                 transpose_add(
@@ -330,12 +329,12 @@ def tile_mug_head_kernel(tc, text_feat, video_feat, text_mask, out):
 
         def pipeline_step(step):
             multiply(step + 1)
-            store_frame_sums(step - SUM_LAG - 1)
             subtract_tops(step)
             weigh(step)
             form_products(step - 1)
             add_up_tokens(step - SUM_LAG)
             add_up_frames(step - SUM_LAG)
+            store_frame_sums(step - SUM_LAG - 1)
 
         with tc.tile_pool(name="text_prep", bufs=2) as text_prep:
             text_raw = text_prep.tile([P, TOKENS, FEATURES], BF16, name="text_raw", bufs=1)
@@ -375,17 +374,19 @@ def tile_mug_head_kernel(tc, text_feat, video_feat, text_mask, out):
                     prepare_text_quad((step + 1) // QUAD + 1)
                 pipeline_step(step)
 
+        with tc.manual_schedule():
+            for step in range(TOKENS - 1, FIRST_STEPS - 1):
+                pipeline_step(step)
+
         finish = pools.enter_context(tc.tile_pool(name="finish", bufs=2))
 
         def turn_back(made, first_col):
-            made["bank"] = psum.tile([P, BLOCKS * P], F32, tag="back", name="turned_back", bufs=1)
+            made["bank"] = psum.tile([P, BLOCKS * P], F32, tag="first", name="turned_back")
             for k in range(BLOCKS):
                 block = sums[:, 1, first_col + k * P : first_col + (k + 1) * P]
                 nc.tensor.transpose(made["bank"][:, k * P : (k + 1) * P], block, ident_f32[:])
 
-        def division_pieces(phase):
-            first_col = token_sum_col(phase - 1) if phase > 0 else 0
-            last_col = frame_sum_col(phase) + FRAME_SUM_COLS if phase < GROUPS else SUM_COLS
+        def division_pieces(first_col, last_col):
             weights = sums[:, 0, first_col:last_col]
 
             def invert():
@@ -403,15 +404,20 @@ def tile_mug_head_kernel(tc, text_feat, video_feat, text_mask, out):
                 pieces.append(lambda col=col: multiply_by_inverse(col))
             return pieces
 
-        def pooled_mean_pieces(made, count, result):
+        def new_statistics(name):
+            return {
+                "top": finish.tile([P, P], F32, name=name + "_top", bufs=1),
+                "weights": finish.tile([P, P], F32, name=name + "_weights", bufs=1),
+                "products": finish.tile([P, P], F32, name=name + "_products", bufs=1),
+            }
+
+        def pooling_pieces(made, count, group, statistics):
             shape = [P, GROUP_VIDEOS, count]
-            small = [P, GROUP_VIDEOS]
+            videos = slice(group * GROUP_VIDEOS, (group + 1) * GROUP_VIDEOS)
+            top = statistics["top"][:, videos]
 
             def find_top():
-                made["top"] = finish.tile(small, F32, tag="top", name="top")
-                nc.vector.tensor_reduce(
-                    out=made["top"][:], in_=made["values"][:], axis=INNERMOST, op=ALU.max
-                )
+                nc.vector.tensor_reduce(out=top, in_=made["values"][:], axis=INNERMOST, op=ALU.max)
 
             def weigh_deviations():
                 made["dev"] = finish.tile(shape, F32, tag="dev%d" % count, name="dev")
@@ -419,7 +425,7 @@ def tile_mug_head_kernel(tc, text_feat, video_feat, text_mask, out):
                 nc.vector.tensor_tensor(
                     out=made["dev"][:],
                     in0=made["values"][:],
-                    in1=made["top"][:].unsqueeze(2).to_broadcast(shape),
+                    in1=top.unsqueeze(2).to_broadcast(shape),
                     op=ALU.subtract,
                 )
                 nc.scalar.activation(out=made["wgt"][:], in_=made["dev"][:], func=FN.Exp, scale=TAU)
@@ -430,79 +436,69 @@ def tile_mug_head_kernel(tc, text_feat, video_feat, text_mask, out):
                 )
 
             def add_weights():
-                made["weight_sum"] = finish.tile(small, F32, tag="weight_sum", name="weight_sum")
                 nc.vector.tensor_reduce(
-                    out=made["weight_sum"][:], in_=made["wgt"][:], axis=INNERMOST, op=ALU.add
+                    out=statistics["weights"][:, videos], in_=made["wgt"][:],
+                    axis=INNERMOST, op=ALU.add,
                 )
 
             def add_products():
-                made["product_sum"] = finish.tile(small, F32, tag="product_sum", name="product_sum")
                 nc.vector.tensor_reduce(
-                    out=made["product_sum"][:], in_=made["dev"][:], axis=INNERMOST, op=ALU.add
+                    out=statistics["products"][:, videos], in_=made["dev"][:],
+                    axis=INNERMOST, op=ALU.add,
                 )
 
-            def divide_and_shift():
-                weight_sum = made["weight_sum"]
-                product_sum = made["product_sum"]
-                nc.vector.reciprocal(out=weight_sum[:], in_=weight_sum[:])
-                nc.vector.tensor_tensor(
-                    out=product_sum[:], in0=product_sum[:], in1=weight_sum[:], op=ALU.mult
-                )
-                nc.vector.tensor_tensor(
-                    out=result, in0=product_sum[:], in1=made["top"][:], op=ALU.add
-                )
+            return [find_top, weigh_deviations, form_product, add_weights, add_products]
 
-            return [
-                find_top, weigh_deviations, form_product, add_weights, add_products, divide_and_shift
-            ]
+        def pooled_mean(statistics):
+            nc.vector.reciprocal(out=statistics["weights"][:], in_=statistics["weights"][:])
+            nc.vector.tensor_tensor(
+                out=statistics["products"][:], in0=statistics["products"][:],
+                in1=statistics["weights"][:], op=ALU.mult,
+            )
+            nc.vector.tensor_tensor(
+                out=statistics["products"][:], in0=statistics["products"][:],
+                in1=statistics["top"][:], op=ALU.add,
+            )
+            return statistics["products"]
 
-        def text_to_video_pieces(group):
+        def text_to_video_pieces(group, statistics):
             made = {}
-            shape = [P, GROUP_VIDEOS, TOKENS]
             tokens_of_bank = BLOCKS * QUAD
 
             def add_frame_top(first):
                 if first == 0:
-                    made["values"] = finish.tile(shape, F32, tag="t2v", name="t2v")
+                    made["raw"] = finish.tile(
+                        [P, TOKENS, GROUP_VIDEOS], F32, tag="t2v_raw", name="t2v_raw"
+                    )
                 tokens = slice(first, first + tokens_of_bank)
                 nc.vector.tensor_tensor(
-                    out=made["values"][:, :, tokens],
-                    in0=made["bank"][:].rearrange("a (t b) -> a b t", b=GROUP_VIDEOS),
-                    in1=frame_top[:, group, tokens, :].rearrange("a t b -> a b t"),
+                    out=made["raw"][:, tokens, :],
+                    in0=made["bank"][:].rearrange("a (t b) -> a t b", b=GROUP_VIDEOS),
+                    in1=frame_top[:, group, tokens, :],
                     op=ALU.add,
                 )
 
-            def apply_mask():
-                nc.vector.tensor_tensor(
-                    out=made["values"][:],
-                    in0=made["values"][:],
-                    in1=mask[:].unsqueeze(1).to_broadcast(shape),
-                    op=ALU.mult,
-                )
-
-            def find_zeros():
-                made["bar"] = finish.tile(shape, F32, tag="bar", name="bar")
-                nc.vector.tensor_scalar(
-                    out=made["bar"][:], in0=made["values"][:], scalar1=0.0, scalar2=BARRED,
-                    op0=ALU.is_equal, op1=ALU.mult,
-                )
-
-            def bar_zeros():
-                nc.vector.tensor_tensor(
-                    out=made["values"][:], in0=made["values"][:], in1=made["bar"][:], op=ALU.add
-                )
+            def mask_and_bar():
+                made["values"] = finish.tile([P, GROUP_VIDEOS, TOKENS], F32, tag="t2v", name="t2v")
+                for token in range(TOKENS):
+                    nc.scalar.activation(
+                        out=made["values"][:, :, token],
+                        in_=made["raw"][:, token, :],
+                        func=FN.Identity,
+                        scale=mask[:, token : token + 1],
+                        bias=barred[:, token : token + 1],
+                    )
 
             pieces = []
             for first in range(0, TOKENS, tokens_of_bank):
                 first_col = frame_sum_col(group) + first // QUAD * P
                 pieces.append(lambda first_col=first_col: turn_back(made, first_col))
                 pieces.append(lambda first=first: add_frame_top(first))
-            pieces.extend([apply_mask, find_zeros, bar_zeros])
-            videos = slice(group * GROUP_VIDEOS, (group + 1) * GROUP_VIDEOS)
-            pieces.extend(pooled_mean_pieces(made, TOKENS, text_to_video[:, videos]))
+            pieces.append(mask_and_bar)
+            pieces.extend(pooling_pieces(made, TOKENS, group, statistics))
             return pieces
 
-        def video_to_text_pieces(group):
+        def video_to_text_pieces(group, statistics):
             made = {}
 
             def add_token_top():
@@ -515,29 +511,42 @@ def tile_mug_head_kernel(tc, text_feat, video_feat, text_mask, out):
                 )
 
             pieces = [lambda: turn_back(made, token_sum_col(group)), add_token_top]
-            videos = slice(group * GROUP_VIDEOS, (group + 1) * GROUP_VIDEOS)
-            pieces.extend(pooled_mean_pieces(made, FRAMES, video_to_text[:, videos]))
+            pieces.extend(pooling_pieces(made, FRAMES, group, statistics))
             return pieces
 
-        piece_after = {}
+        over_tokens = new_statistics("over_tokens")
+        over_frames = new_statistics("over_frames")
+        last_phase_col = token_sum_col(GROUPS - 2)
+        waiting = []
+        for piece in division_pieces(0, last_phase_col):
+            waiting.append((FIRST_STEPS - 1, piece))
         for phase in range(GROUPS + 1):
-            pieces = division_pieces(phase)
+            ready = max(FIRST_STEPS - 1, (phase + 1) * TOKENS + SUM_LAG)
+            pieces = []
+            if phase == GROUPS - 1:
+                pieces.extend(division_pieces(last_phase_col, token_sum_col(GROUPS - 1)))
+            if phase == GROUPS:
+                pieces.extend(division_pieces(token_sum_col(GROUPS - 1), SUM_COLS))
             if phase < GROUPS:
-                pieces.extend(text_to_video_pieces(phase))
+                pieces.extend(text_to_video_pieces(phase, over_tokens))
             if phase > 0:
-                pieces.extend(video_to_text_pieces(phase - 1))
-            assert len(pieces) <= TOKENS
-            for k, piece in enumerate(pieces):
-                piece_after[(phase + 1) * TOKENS + SUM_LAG + k] = piece
+                pieces.extend(video_to_text_pieces(phase - 1, over_frames))
+            for piece in pieces:
+                waiting.append((ready, piece))
 
-        for step in range(TOKENS - 1, max(piece_after) + 1):
+        served = 0
+        for step in range(FIRST_STEPS - 1, STEPS + SUM_LAG + 1):
             pipeline_step(step)
-            if step in piece_after:
-                piece_after[step]()
+            for turn in range(PIECES_PER_STEP):
+                if served < len(waiting) and waiting[served][0] <= step:
+                    waiting[served][1]()
+                    served += 1
+        for ready, piece in waiting[served:]:
+            piece()
 
         result = finish.tile([P, P], F32, name="result", bufs=1)
         nc.vector.tensor_tensor(
-            out=result[:], in0=text_to_video[:], in1=video_to_text[:], op=ALU.add
+            out=result[:], in0=pooled_mean(over_tokens)[:], in1=pooled_mean(over_frames)[:], op=ALU.add
         )
         nc.vector.tensor_scalar_mul(out=result[:], in0=result[:], scalar1=0.5)
         nc.sync.dma_start(out=out, in_=result[:])

from contextlib import ExitStack

import concourse.mybir as mybir
from concourse.masks import make_identity

F32 = mybir.dt.float32
BF16 = mybir.dt.bfloat16
U32 = mybir.dt.uint32
U8 = mybir.dt.uint8
FP8X4 = mybir.dt.float8_e4m3fn_x4
ALU = mybir.AluOpType
FN = mybir.ActivationFunctionType
INNERMOST = mybir.AxisListType.X

P = 128
TOKENS = 32
FRAMES = 16
FEATURES = 512
PACK = 4
TAU = 100.0
EPS = 1.0e-6
BARRED = -1.0e30

GROUPS = 4
GROUP_VIDEOS = P // GROUPS
GROUP_COLS = FRAMES * GROUP_VIDEOS
BLOCKS = GROUP_COLS // P
QUAD = 4
QUADS = TOKENS // QUAD
FRAME_SUM_COLS = QUADS * P
PHASE_SUM_COLS = GROUP_COLS + FRAME_SUM_COLS
SUM_COLS = GROUPS * PHASE_SUM_COLS

FIRST_STEPS = GROUPS * TOKENS
STEPS = FIRST_STEPS + TOKENS
FIRST_SWEEP_PASSES = 2
PAIR = 2
SUM_LAG = 4
PIECES_PER_STEP = 2

FLOPS = 2 * (P * TOKENS) * (P * FRAMES) * FEATURES


def tile_mug_head_kernel(tc, text_feat, video_feat, text_mask, out):
    nc = tc.nc
    with ExitStack() as pools:
        consts = pools.enter_context(tc.tile_pool(name="consts", bufs=1))
        keep = pools.enter_context(tc.tile_pool(name="keep", bufs=1))
        psum = pools.enter_context(tc.psum_pool(name="psum", bufs=2))

        ident_f32 = consts.tile([P, P], F32, name="ident_f32")
        make_identity(nc, ident_f32[:])
        ident_bf16 = consts.tile([P, P], BF16, name="ident_bf16")
        make_identity(nc, ident_bf16[:])

        mask_bf16 = consts.tile([P, TOKENS], BF16, name="mask_bf16")
        nc.sync.dma_start(out=mask_bf16[:], in_=text_mask)
        mask = consts.tile([P, TOKENS], F32, name="mask")
        nc.vector.tensor_copy(out=mask[:], in_=mask_bf16[:])
        sharp_mask = consts.tile([P, TOKENS], F32, name="sharp_mask")
        nc.vector.tensor_scalar_mul(out=sharp_mask[:], in0=mask[:], scalar1=TAU)
        barred = consts.tile([P, TOKENS], F32, name="barred")
        nc.vector.tensor_scalar(
            out=barred[:], in0=mask[:], scalar1=0.0, scalar2=BARRED, op0=ALU.is_equal, op1=ALU.mult
        )
        mask_top = consts.tile([P, 1], F32, name="mask_top")
        nc.vector.tensor_reduce(out=mask_top[:], in_=mask[:], axis=INNERMOST, op=ALU.max)

        text_codes = keep.tile([P, TOKENS * P], U32, name="text_codes", align_bytes=64)
        text_scales = keep.tile([P, TOKENS * P], U8, name="text_scales", align_bytes=64)
        video_codes = keep.tile([P, GROUPS * GROUP_COLS], U32, name="video_codes", align_bytes=64)
        video_scales = keep.tile([P, GROUPS * GROUP_COLS], U8, name="video_scales", align_bytes=64)
        frame_top = keep.tile([P, GROUPS, TOKENS, GROUP_VIDEOS], F32, name="frame_top")
        token_top = keep.tile([P, GROUPS, GROUP_COLS], F32, name="token_top")
        sums = keep.tile([P, 2, SUM_COLS], F32, name="sums")

        def transpose_add(acc, block, start, stop):
            nc.tensor.matmul(
                out=acc, lhsT=block, rhs=ident_f32[:], is_transpose=True, start=start, stop=stop
            )

        def inverse_norms(pool, raw, count):
            by_scalar = pool.tile([P, count // 2], F32, name="squares_by_scalar", bufs=1)
            by_vector = pool.tile([P, count // 2], F32, name="squares_by_vector", bufs=1)
            for i in range(count):
                total = slice(i // 2, i // 2 + 1)
                if i % 2 == 0:
                    squares = pool.tile([P, FEATURES], BF16, tag="squares_s", name="squares_s")
                    nc.scalar.activation(
                        out=squares[:], in_=raw[:, i, :], func=FN.Square, accum_out=by_scalar[:, total]
                    )
                else:
                    squares = pool.tile([P, FEATURES], F32, tag="squares_v", name="squares_v")
                    nc.vector.scalar_tensor_tensor(
                        out=squares[:], in0=raw[:, i, :], scalar=1.0, in1=raw[:, i, :],
                        op0=ALU.mult, op1=ALU.mult, accum_out=by_vector[:, total],
                    )
            inverse = pool.tile([P, 2, count // 2], F32, name="inverse", bufs=1)
            for parity, square_sum in enumerate((by_scalar, by_vector)):
                nc.vector.tensor_scalar_max(out=square_sum[:], in0=square_sum[:], scalar1=EPS * EPS)
                nc.scalar.sqrt(out=inverse[:, parity, :], in_=square_sum[:])
                nc.vector.reciprocal(out=inverse[:, parity, :], in_=inverse[:, parity, :])
            return inverse

        def features_to_partitions(rows):
            bank = psum.tile([P, PACK, P], BF16, tag="second", name="turned_rows")
            for j in range(PACK):
                nc.tensor.transpose(bank[:, j, :], rows[:, j * P : (j + 1) * P], ident_bf16[:])
            return bank

        with tc.tile_pool(name="video_prep", bufs=2) as video_prep:
            video_raw = video_prep.tile([P, FRAMES, FEATURES], BF16, name="video_raw", bufs=1)
            for first in range(0, FRAMES, 4):
                nc.sync.dma_start(
                    out=video_raw[:, first : first + 4, :], in_=video_feat[:, first : first + 4, :]
                )
            warm = video_prep.tile([P, 1], F32, name="warm", bufs=1)
            nc.vector.memset(warm[:], 1.0)
            nc.scalar.sqrt(out=warm[:], in_=warm[:])
            video_inverse = inverse_norms(video_prep, video_raw, FRAMES)
            video_grouped = video_prep.tile(
                [P, GROUPS, FRAMES, GROUP_VIDEOS, PACK], BF16,
                name="video_grouped", bufs=1, align_bytes=64,
            )
            for v in range(FRAMES):
                rows = video_prep.tile([P, FEATURES], BF16, tag="rows", name="rows", bufs=3)
                nc.vector.tensor_scalar_mul(
                    out=rows[:],
                    in0=video_raw[:, v, :],
                    scalar1=video_inverse[:, v % 2, v // 2 : v // 2 + 1],
                )
                bank = features_to_partitions(rows)
                copy = nc.scalar.copy if v % 2 == 0 else nc.vector.tensor_copy
                copy(
                    out=video_grouped[:, :, v, :, :],
                    in_=bank[:].rearrange("p j (g b) -> p g b j", g=GROUPS),
                )
            for group in range(GROUPS):
                cols = slice(group * GROUP_COLS, (group + 1) * GROUP_COLS)
                nc.vector.quantize_mx(
                    out=video_codes[:, cols].bitcast(FP8X4),
                    scales=video_scales[:, cols],
                    in_=video_grouped[:, group, :, :, :].rearrange("p v b j -> p (v b j)"),
                )

        quad_work = pools.enter_context(tc.tile_pool(name="quad_work", bufs=3))
        pair_work = pools.enter_context(tc.tile_pool(name="pair_work", bufs=3))

        def similarities(token, group, tag, times):
            sim = psum.tile([P, GROUP_COLS], F32, tag=tag, name="sim")
            texts = slice(token * P, (token + 1) * P)
            cols = slice(group * GROUP_COLS, (group + 1) * GROUP_COLS)
            for repeat in range(times):
                nc.tensor.matmul_mx(
                    out=sim[:],
                    lhsT=text_codes[:, texts].bitcast(FP8X4),
                    lhsT_scale=text_scales[:, texts],
                    rhs=video_codes[:, cols].bitcast(FP8X4),
                    rhs_scale=video_scales[:, cols],
                    start=True,
                    stop=True,
                )
            return sim

        sim_first = {}
        sim_second = {}
        frame_tiles = {}
        token_tiles = {}
        quad_banks = {}
        group_banks = {}

        def frame_sum_col(group):
            return group * PHASE_SUM_COLS

        def token_sum_col(group):
            return (group + 1) * PHASE_SUM_COLS - GROUP_COLS

        def in_first_sweep(step):
            return 0 <= step < FIRST_STEPS

        def in_second_sweep(step):
            return TOKENS <= step < STEPS

        def multiply(step):
            token = step % TOKENS
            if in_first_sweep(step):
                sim_first[step] = similarities(token, step // TOKENS, "first", FIRST_SWEEP_PASSES)
            if in_second_sweep(step):
                sim_second[step] = similarities(token, step // TOKENS - 1, "second", 1)

        def subtract_tops(step):
            token = step % TOKENS
            group = step // TOKENS
            top_f = None
            if in_first_sweep(step):
                top_f = frame_top[:, group, token, :]
                nc.vector.tensor_reduce(
                    out=top_f,
                    in_=sim_first[step][:].rearrange("a (v b) -> a b v", v=FRAMES),
                    axis=INNERMOST,
                    op=ALU.max,
                )
            if in_second_sweep(step):
                if step % PAIR == 0:
                    pair_shape = [P, PAIR, GROUP_COLS]
                    token_tiles[step // PAIR] = (
                        pair_work.tile(pair_shape, F32, tag="dev_t", name="dev_t"),
                        pair_work.tile(pair_shape, F32, tag="wgt_t", name="wgt_t"),
                    )
                nc.vector.scalar_tensor_tensor(
                    out=token_tiles[step // PAIR][0][:, step % PAIR, :],
                    in0=sim_second[step][:],
                    scalar=mask[:, token : token + 1],
                    in1=token_top[:, group - 1, :],
                    op0=ALU.mult,
                    op1=ALU.subtract,
                )
            if in_first_sweep(step):
                sim = sim_first[step]
                if step % QUAD == 0:
                    quad_shape = [P, FRAMES, QUAD, GROUP_VIDEOS]
                    frame_tiles[step // QUAD] = (
                        quad_work.tile(quad_shape, F32, tag="dev_f", name="dev_f"),
                        quad_work.tile(quad_shape, F32, tag="wgt_f", name="wgt_f"),
                    )
                nc.vector.tensor_tensor(
                    out=frame_tiles[step // QUAD][0][:, :, step % QUAD, :],
                    in0=sim[:].rearrange("a (v b) -> a v b", v=FRAMES),
                    in1=top_f.unsqueeze(1).to_broadcast([P, FRAMES, GROUP_VIDEOS]),
                    op=ALU.subtract,
                )
                bar = barred[:, token : token + 1]
                top_t = token_top[:, group, :]
                if token == 0:
                    nc.vector.tensor_scalar(
                        out=top_t, in0=sim[:], scalar1=bar, scalar2=None, op0=ALU.add
                    )
                else:
                    nc.vector.scalar_tensor_tensor(
                        out=top_t, in0=sim[:], scalar=bar, in1=top_t, op0=ALU.add, op1=ALU.max
                    )
                if token == TOKENS - 1:
                    nc.vector.tensor_scalar_mul(out=top_t, in0=top_t, scalar1=mask_top[:, 0:1])

        def weigh(step):
            token = step % TOKENS
            if in_second_sweep(step):
                dev_t, wgt_t = token_tiles[step // PAIR]
                nc.scalar.activation(
                    out=wgt_t[:, step % PAIR, :],
                    in_=dev_t[:, step % PAIR, :],
                    func=FN.Exp,
                    scale=TAU,
                    bias=barred[:, token : token + 1],
                )
            if in_first_sweep(step):
                dev_f, wgt_f = frame_tiles[step // QUAD]
                nc.scalar.activation(
                    out=wgt_f[:, :, step % QUAD, :],
                    in_=dev_f[:, :, step % QUAD, :],
                    func=FN.Exp,
                    scale=sharp_mask[:, token : token + 1],
                )

        def form_products(step):
            if step % PAIR != PAIR - 1:
                return
            if in_second_sweep(step):
                dev_t, wgt_t = token_tiles[step // PAIR]
                nc.gpsimd.tensor_tensor(out=dev_t[:], in0=dev_t[:], in1=wgt_t[:], op=ALU.mult)
            if in_first_sweep(step):
                dev_f, wgt_f = frame_tiles[step // QUAD]
                slots = slice(step % QUAD - (PAIR - 1), step % QUAD + 1)
                nc.gpsimd.tensor_tensor(
                    out=dev_f[:, :, slots, :],
                    in0=dev_f[:, :, slots, :],
                    in1=wgt_f[:, :, slots, :],
                    op=ALU.mult,
                )

        def add_up_tokens(step):
            if not in_second_sweep(step):
                return
            token = step % TOKENS
            group = step // TOKENS - 1
            if token == 0:
                group_banks[group] = (
                    psum.tile([P, GROUP_COLS], F32, tag="weight_sums", name="weight_sums", bufs=1),
                    psum.tile([P, GROUP_COLS], F32, tag="product_sums", name="product_sums", bufs=1),
                )
            dev_t, wgt_t = token_tiles[step // PAIR]
            for plane, terms in enumerate((wgt_t, dev_t)):
                acc = group_banks[group][plane]
                for k in range(BLOCKS):
                    cols = slice(k * P, (k + 1) * P)
                    transpose_add(
                        acc[:, cols],
                        terms[:, step % PAIR, cols],
                        token == 0 and k == 0,
                        token == TOKENS - 1 and k == BLOCKS - 1,
                    )
                if token == TOKENS - 1:
                    first_col = token_sum_col(group)
                    nc.scalar.copy(out=sums[:, plane, first_col : first_col + GROUP_COLS], in_=acc[:])

        def add_up_frames(step):
            if not in_first_sweep(step):
                return
            quad = step // QUAD
            plane = (step % QUAD) // 2
            first_frame = (step % 2) * (FRAMES // 2)
            if step % QUAD == 0:
                quad_banks[quad] = psum.tile([P, 2, P], F32, tag="quad_sums", name="quad_sums")
            terms = frame_tiles[quad][1 - plane]
            for v in range(first_frame, first_frame + FRAMES // 2):
                transpose_add(
                    quad_banks[quad][:, plane, :],
                    terms[:, v, :, :].rearrange("a s b -> a (s b)"),
                    v == 0,
                    v == FRAMES - 1,
                )

        def store_frame_sums(step):
            if in_first_sweep(step) and step % QUAD == QUAD - 1:
                first_col = frame_sum_col(step // TOKENS) + (step % TOKENS) // QUAD * P
                nc.scalar.copy(
                    out=sums[:, :, first_col : first_col + P], in_=quad_banks[step // QUAD][:]
                )

        def pipeline_step(step):
            multiply(step + 1)
            subtract_tops(step)
            weigh(step)
            form_products(step - 1)
            add_up_tokens(step - SUM_LAG)
            add_up_frames(step - SUM_LAG)
            store_frame_sums(step - SUM_LAG - 1)

        with tc.tile_pool(name="text_prep", bufs=2) as text_prep:
            text_raw = text_prep.tile([P, TOKENS, FEATURES], BF16, name="text_raw", bufs=1)
            for first in range(0, TOKENS, 8):
                nc.sync.dma_start(
                    out=text_raw[:, first : first + 8, :], in_=text_feat[:, first : first + 8, :]
                )
            text_inverse = inverse_norms(text_prep, text_raw, TOKENS)

            def prepare_text_quad(quad):
                grouped = text_prep.tile(
                    [P, QUAD, P, PACK], BF16, tag="text_grouped", name="text_grouped", align_bytes=64
                )
                for slot in range(QUAD):
                    token = quad * QUAD + slot
                    rows = text_prep.tile([P, FEATURES], BF16, tag="rows", name="rows", bufs=3)
                    nc.scalar.activation(
                        out=rows[:],
                        in_=text_raw[:, token, :],
                        func=FN.Copy,
                        scale=text_inverse[:, token % 2, token // 2 : token // 2 + 1],
                    )
                    bank = features_to_partitions(rows)
                    nc.scalar.copy(
                        out=grouped[:, slot, :, :], in_=bank[:].rearrange("p j a -> p a j")
                    )
                cols = slice(quad * QUAD * P, (quad + 1) * QUAD * P)
                nc.vector.quantize_mx(
                    out=text_codes[:, cols].bitcast(FP8X4),
                    scales=text_scales[:, cols],
                    in_=grouped[:].rearrange("p s a j -> p (s a j)"),
                )

            prepare_text_quad(0)
            for step in range(-1, TOKENS - 1):
                if (step + 1) % QUAD == 0 and step + 1 + QUAD < TOKENS:
                    prepare_text_quad((step + 1) // QUAD + 1)
                pipeline_step(step)

        with tc.manual_schedule():
            for step in range(TOKENS - 1, FIRST_STEPS - 1):
                pipeline_step(step)

        finish = pools.enter_context(tc.tile_pool(name="finish", bufs=2))

        def turn_back(made, first_col):
            made["bank"] = psum.tile([P, BLOCKS * P], F32, tag="first", name="turned_back")
            for k in range(BLOCKS):
                block = sums[:, 1, first_col + k * P : first_col + (k + 1) * P]
                nc.tensor.transpose(made["bank"][:, k * P : (k + 1) * P], block, ident_f32[:])

        def division_pieces(first_col, last_col):
            weights = sums[:, 0, first_col:last_col]

            def invert():
                nc.scalar.activation(out=weights, in_=weights, func=FN.Ln)
                nc.scalar.activation(out=weights, in_=weights, func=FN.Exp, scale=-1.0)

            def multiply_by_inverse(col):
                cols = slice(col, col + GROUP_COLS)
                nc.gpsimd.tensor_tensor(
                    out=sums[:, 1, cols], in0=sums[:, 1, cols], in1=sums[:, 0, cols], op=ALU.mult
                )

            pieces = [invert]
            for col in range(first_col, last_col, GROUP_COLS):
                pieces.append(lambda col=col: multiply_by_inverse(col))
            return pieces

        def new_statistics(name):
            return {
                "top": finish.tile([P, P], F32, name=name + "_top", bufs=1),
                "weights": finish.tile([P, P], F32, name=name + "_weights", bufs=1),
                "products": finish.tile([P, P], F32, name=name + "_products", bufs=1),
            }

        def pooling_pieces(made, count, group, statistics):
            shape = [P, GROUP_VIDEOS, count]
            videos = slice(group * GROUP_VIDEOS, (group + 1) * GROUP_VIDEOS)
            top = statistics["top"][:, videos]

            def find_top():
                nc.vector.tensor_reduce(out=top, in_=made["values"][:], axis=INNERMOST, op=ALU.max)

            def weigh_deviations():
                made["dev"] = finish.tile(shape, F32, tag="dev%d" % count, name="dev")
                made["wgt"] = finish.tile(shape, F32, tag="wgt%d" % count, name="wgt")
                nc.vector.tensor_tensor(
                    out=made["dev"][:],
                    in0=made["values"][:],
                    in1=top.unsqueeze(2).to_broadcast(shape),
                    op=ALU.subtract,
                )
                nc.scalar.activation(out=made["wgt"][:], in_=made["dev"][:], func=FN.Exp, scale=TAU)

            def form_product():
                nc.gpsimd.tensor_tensor(
                    out=made["dev"][:], in0=made["dev"][:], in1=made["wgt"][:], op=ALU.mult
                )

            def add_weights():
                nc.vector.tensor_reduce(
                    out=statistics["weights"][:, videos], in_=made["wgt"][:],
                    axis=INNERMOST, op=ALU.add,
                )

            def add_products():
                nc.vector.tensor_reduce(
                    out=statistics["products"][:, videos], in_=made["dev"][:],
                    axis=INNERMOST, op=ALU.add,
                )

            return [find_top, weigh_deviations, form_product, add_weights, add_products]

        def pooled_mean(statistics):
            nc.vector.reciprocal(out=statistics["weights"][:], in_=statistics["weights"][:])
            nc.vector.tensor_tensor(
                out=statistics["products"][:], in0=statistics["products"][:],
                in1=statistics["weights"][:], op=ALU.mult,
            )
            nc.vector.tensor_tensor(
                out=statistics["products"][:], in0=statistics["products"][:],
                in1=statistics["top"][:], op=ALU.add,
            )
            return statistics["products"]

        def text_to_video_pieces(group, statistics):
            made = {}
            tokens_of_bank = BLOCKS * QUAD

            def add_frame_top(first):
                if first == 0:
                    made["raw"] = finish.tile(
                        [P, TOKENS, GROUP_VIDEOS], F32, tag="t2v_raw", name="t2v_raw"
                    )
                tokens = slice(first, first + tokens_of_bank)
                nc.vector.tensor_tensor(
                    out=made["raw"][:, tokens, :],
                    in0=made["bank"][:].rearrange("a (t b) -> a t b", b=GROUP_VIDEOS),
                    in1=frame_top[:, group, tokens, :],
                    op=ALU.add,
                )

            def mask_and_bar():
                made["values"] = finish.tile([P, GROUP_VIDEOS, TOKENS], F32, tag="t2v", name="t2v")
                for token in range(TOKENS):
                    nc.scalar.activation(
                        out=made["values"][:, :, token],
                        in_=made["raw"][:, token, :],
                        func=FN.Identity,
                        scale=mask[:, token : token + 1],
                        bias=barred[:, token : token + 1],
                    )

            pieces = []
            for first in range(0, TOKENS, tokens_of_bank):
                first_col = frame_sum_col(group) + first // QUAD * P
                pieces.append(lambda first_col=first_col: turn_back(made, first_col))
                pieces.append(lambda first=first: add_frame_top(first))
            pieces.append(mask_and_bar)
            pieces.extend(pooling_pieces(made, TOKENS, group, statistics))
            return pieces

        def video_to_text_pieces(group, statistics):
            made = {}

            def add_token_top():
                made["values"] = finish.tile([P, GROUP_VIDEOS, FRAMES], F32, tag="v2t", name="v2t")
                nc.vector.tensor_tensor(
                    out=made["values"][:],
                    in0=made["bank"][:].rearrange("a (v b) -> a b v", v=FRAMES),
                    in1=token_top[:, group, :].rearrange("a (v b) -> a b v", v=FRAMES),
                    op=ALU.add,
                )

            pieces = [lambda: turn_back(made, token_sum_col(group)), add_token_top]
            pieces.extend(pooling_pieces(made, FRAMES, group, statistics))
            return pieces

        over_tokens = new_statistics("over_tokens")
        over_frames = new_statistics("over_frames")
        last_phase_col = token_sum_col(GROUPS - 2)
        waiting = []
        for piece in division_pieces(0, last_phase_col):
            waiting.append((FIRST_STEPS - 1, piece))
        for phase in range(GROUPS + 1):
            ready = max(FIRST_STEPS - 1, (phase + 1) * TOKENS + SUM_LAG)
            pieces = []
            if phase == GROUPS - 1:
                pieces.extend(division_pieces(last_phase_col, token_sum_col(GROUPS - 1)))
            if phase == GROUPS:
                pieces.extend(division_pieces(token_sum_col(GROUPS - 1), SUM_COLS))
            if phase < GROUPS:
                pieces.extend(text_to_video_pieces(phase, over_tokens))
            if phase > 0:
                pieces.extend(video_to_text_pieces(phase - 1, over_frames))
            for piece in pieces:
                waiting.append((ready, piece))

        served = 0
        for step in range(FIRST_STEPS - 1, STEPS + SUM_LAG + 1):
            pipeline_step(step)
            for turn in range(PIECES_PER_STEP):
                if served < len(waiting) and waiting[served][0] <= step:
                    waiting[served][1]()
                    served += 1
        for ready, piece in waiting[served:]:
            piece()

        result = finish.tile([P, P], F32, name="result", bufs=1)
        nc.vector.tensor_tensor(
            out=result[:], in0=pooled_mean(over_tokens)[:], in1=pooled_mean(over_frames)[:], op=ALU.add
        )
        nc.vector.tensor_scalar_mul(out=result[:], in0=result[:], scalar1=0.5)
        nc.sync.dma_start(out=out, in_=result[:])
